import numpy as np
import ml_dtypes


def mxq(x, axis, fmt="e4m3"):
    dtype, down = {"e4m3": (ml_dtypes.float8_e4m3fn, 7), "e5m2": (ml_dtypes.float8_e5m2, 14)}[fmt]
    v = np.moveaxis(np.asarray(x, np.float32).astype(ml_dtypes.bfloat16).astype(np.float64), axis, -1)
    blocks = v.reshape(v.shape[:-1] + (-1, 32))
    amax = np.abs(blocks).max(-1, keepdims=True)
    byte = np.maximum(np.where(amax > 0, np.frexp(amax)[1] - 1 + 127, 0) - down, 1)
    scale = np.exp2(byte - 127.0)
    codes = (blocks / scale).astype(np.float32).astype(dtype).astype(np.float64)
    return np.moveaxis((codes * scale).reshape(v.shape), -1, axis)


BF16 = ml_dtypes.bfloat16


def bf(x):
    return np.asarray(x, np.float32).astype(BF16)


def f64(x):
    return np.asarray(x).astype(np.float64)


N, CK, CV, T, H, W = 32, 128, 128, 2, 16, 16
Q = H * W
M = T * Q


def setup_inputs():
    return {"q_key": bf(np.random.standard_normal((N, CK, H, W))),
            "q_val": bf(np.random.standard_normal((N, CV, H, W))),
            "m_key": bf(np.random.standard_normal((N, CK, T, H, W))),
            "m_val": bf(np.random.standard_normal((N, CV, T, H, W)) * 0.5 * Q / np.sqrt(M))}


def reference(q_key, q_val, m_key, m_val):
    qk = f64(q_key).reshape(N, CK, Q)
    mk = f64(m_key).reshape(N, CK, M)
    aff = (qk.transpose(0, 2, 1) @ mk) * (CK ** -0.5)
    e = np.exp(aff - aff.max(axis=1, keepdims=True))
    attn = e / e.sum(axis=1, keepdims=True)
    mv = f64(m_val).reshape(N, CV, M)
    mapped = (mxq(mv, 2, "e4m3") @ mxq(attn, 2, "e4m3").transpose(0, 2, 1)).reshape(N, CV, H, W)
    return np.concatenate([f64(q_val), mapped], axis=1)

@@ -1,0 +1,134 @@
+from contextlib import ExitStack
+
+import concourse.mybir as mybir
+from concourse.masks import make_identity
+
+FP8X4 = mybir.dt.float8_e4m3fn_x4
+BF16 = mybir.dt.bfloat16
+F32 = mybir.dt.float32
+U32 = mybir.dt.uint32
+U8 = mybir.dt.uint8
+ALU = mybir.AluOpType
+ACT = mybir.ActivationFunctionType
+AX = mybir.AxisListType
+
+N, C, Q, M = 32, 128, 256, 512
+P = 128
+SCALE = 128 ** -0.5
+FLOPS = 2 * (2 * N * Q * M * C)
+CHUNKS = [2, 2, 4, 4, 4, 4, 4, 4, 4]
+
+
+def tile_stm_head_t_kernel(tc, q_key, q_val, m_key, m_val, out):
+    nc = tc.nc
+    qk_d = q_key.rearrange("n c h w -> c n (h w)")
+    qv_d = q_val.rearrange("n c h w -> c n (h w)")
+    mk_d = m_key.rearrange("n c t h w -> c n (t h w)")
+    mv_d = m_val.rearrange("n c t h w -> c n (t h w)")
+    out_d = out.rearrange("n (g c) h w -> c n g (h w)", g=2)
+
+    with ExitStack() as ctx:
+        keep = ctx.enter_context(tc.tile_pool(name="keep", bufs=1))
+        work = ctx.enter_context(tc.tile_pool(name="work", bufs=4))
+        small = ctx.enter_context(tc.tile_pool(name="small", bufs=6))
+        ps_aff = ctx.enter_context(tc.psum_pool(name="ps_aff", bufs=6))
+        ps_xt = ctx.enter_context(tc.psum_pool(name="ps_xt", bufs=1))
+        ps_mo = ctx.enter_context(tc.psum_pool(name="ps_mo", bufs=1))
+
+        ident = keep.tile([P, P], F32, name="ident")
+        make_identity(nc, ident[:])
+
+        place = {}
+        n0 = 0
+        for ci, size in enumerate(CHUNKS):
+            mk_t = keep.tile([P, size, M], BF16, name="mk%d" % ci)
+            qk_t = keep.tile([P, size, Q], BF16, name="qk%d" % ci)
+            mv_t = keep.tile([P, size, M], BF16, name="mv%d" % ci)
+            qv_t = keep.tile([P, size, Q], BF16, name="qv%d" % ci)
+            nc.sync.dma_start(out=mk_t[:], in_=mk_d[:, n0:n0 + size, :])
+            nc.sync.dma_start(out=qk_t[:], in_=qk_d[:, n0:n0 + size, :])
+            nc.sync.dma_start(out=mv_t[:], in_=mv_d[:, n0:n0 + size, :])
+            nc.sync.dma_start(out=qv_t[:], in_=qv_d[:, n0:n0 + size, :])
+            for i in range(size):
+                place[n0 + i] = (mk_t, qk_t, mv_t, qv_t, i)
+            n0 += size
+
+        vcodes = keep.tile([P, N, C], U32, name="vcodes", align_bytes=64)
+        vscales = keep.tile([P, N, C], U8, name="vscales", align_bytes=64)
+
+        for pr in range(N // 2):
+            xt = ps_xt.tile([P, 2, 2, C], F32)
+            for j in range(2):
+                mk_t, qk_t, mv_t, qv_t, i = place[2 * pr + j]
+                words = mv_t[:].bitcast(F32)
+                for u in range(2):
+                    nc.tensor.transpose(xt[:, j, u, :], words[:, i, 128 * u:128 * (u + 1)], ident[:])
+            vgrp = work.tile([P, 2, C, 4], BF16, align_bytes=64)
+            nc.scalar.copy(out=vgrp[:].bitcast(F32), in_=xt[:].rearrange("p j u c -> p j c u"))
+            nc.vector.quantize_mx(
+                out=vcodes[:, 2 * pr:2 * pr + 2, :].rearrange("p j c -> p (j c)").bitcast(FP8X4),
+                scales=vscales[:, 2 * pr:2 * pr + 2, :].rearrange("p j c -> p (j c)"),
+                in_=vgrp[:].rearrange("p j c t -> p (j c t)"),
+            )
+
+            res = work.tile([P, 2, 2, Q], F32)
+            mo = ps_mo.tile([P, 2, Q], F32)
+            for j in range(2):
+                n = 2 * pr + j
+                mk_t, qk_t, mv_t, qv_t, i = place[n]
+                mx = small.tile([P, 4], F32)
+                nb = small.tile([P, 4], F32)
+                sums = small.tile([P, 4], F32)
+                rs = small.tile([P, 4], F32)
+                ex = work.tile([P, 4, Q], F32)
+                affs = []
+                for u in range(2):
+                    aff = ps_aff.tile([P, 2, Q], F32)
+                    for b in range(2):
+                        nc.tensor.matmul(
+                            out=aff[:, b, :],
+                            lhsT=mk_t[:, i, 256 * u + b:256 * (u + 1):2],
+                            rhs=qk_t[:, i, :],
+                            start=True,
+                            stop=True,
+                        )
+                    nc.vector.tensor_reduce(out=mx[:, 2 * u:2 * u + 2], in_=aff[:], axis=AX.X, op=ALU.max)
+                    affs.append(aff)
+                nc.scalar.mul(out=nb[:], in_=mx[:], mul=-SCALE)
+                for t in range(4):
+                    nc.scalar.activation(
+                        out=ex[:, t, :],
+                        in_=affs[t // 2][:, t % 2, :],
+                        func=ACT.Exp,
+                        bias=nb[:, t:t + 1],
+                        scale=SCALE,
+                        accum_out=sums[:, t:t + 1],
+                    )
+                nc.vector.reciprocal(out=rs[:], in_=sums[:])
+                grp = work.tile([P, Q, 4], BF16, align_bytes=64)
+                nc.vector.tensor_tensor(
+                    out=grp[:],
+                    in0=ex[:].rearrange("p t q -> p q t"),
+                    in1=rs[:].unsqueeze(1).to_broadcast([P, Q, 4]),
+                    op=ALU.mult,
+                )
+                ac = work.tile([P, Q], U32, align_bytes=64)
+                asc = work.tile([P, Q], U8, align_bytes=64)
+                nc.vector.quantize_mx(
+                    out=ac[:].bitcast(FP8X4),
+                    scales=asc[:],
+                    in_=grp[:].rearrange("p q t -> p (q t)"),
+                )
+                nc.tensor.matmul_mx(
+                    out=mo[:, j, :],
+                    lhsT=vcodes[:, n, :].bitcast(FP8X4),
+                    lhsT_scale=vscales[:, n, :],
+                    rhs=ac[:].bitcast(FP8X4),
+                    rhs_scale=asc[:],
+                    start=True,
+                    stop=True,
+                )
+            mk_t, qk_t, mv_t, qv_t, i = place[2 * pr]
+            nc.scalar.copy(out=res[:, :, 1, :], in_=mo[:])
+            nc.scalar.copy(out=res[:, :, 0, :], in_=qv_t[:, i:i + 2, :])
+            nc.sync.dma_start(out=out_d[:, 2 * pr:2 * pr + 2, :, :], in_=res[:])

@@ -17,6 +17,9 @@ P = 128
 SCALE = 128 ** -0.5
 FLOPS = 2 * (2 * N * Q * M * C)
 CHUNKS = [2, 2, 4, 4, 4, 4, 4, 4, 4]
+FIRST = 4
+GQ = 0
+RUN = 4
 
 
 def tile_stm_head_t_kernel(tc, q_key, q_val, m_key, m_val, out):
@@ -34,13 +37,19 @@ def tile_stm_head_t_kernel(tc, q_key, q_val, m_key, m_val, out):
         ps_aff = ctx.enter_context(tc.psum_pool(name="ps_aff", bufs=6))
         ps_xt = ctx.enter_context(tc.psum_pool(name="ps_xt", bufs=1))
         ps_mo = ctx.enter_context(tc.psum_pool(name="ps_mo", bufs=1))
+        ctx.enter_context(tc.manual_schedule())
 
         ident = keep.tile([P, P], F32, name="ident")
         make_identity(nc, ident[:])
+        vcodes = keep.tile([P, N, C], U32, name="vcodes", align_bytes=64)
+        vscales = keep.tile([P, N, C], U8, name="vscales", align_bytes=64)
 
         place = {}
-        n0 = 0
-        for ci, size in enumerate(CHUNKS):
+        starts = [sum(CHUNKS[:ci]) for ci in range(len(CHUNKS))]
+
+        def load(ci):
+            size = CHUNKS[ci]
+            n0 = starts[ci]
             mk_t = keep.tile([P, size, M], BF16, name="mk%d" % ci)
             qk_t = keep.tile([P, size, Q], BF16, name="qk%d" % ci)
             mv_t = keep.tile([P, size, M], BF16, name="mv%d" % ci)
@@ -51,84 +60,154 @@ def tile_stm_head_t_kernel(tc, q_key, q_val, m_key, m_val, out):
             nc.sync.dma_start(out=qv_t[:], in_=qv_d[:, n0:n0 + size, :])
             for i in range(size):
                 place[n0 + i] = (mk_t, qk_t, mv_t, qv_t, i)
-            n0 += size
 
-        vcodes = keep.tile([P, N, C], U32, name="vcodes", align_bytes=64)
-        vscales = keep.tile([P, N, C], U8, name="vscales", align_bytes=64)
+        for ci in range(FIRST):
+            load(ci)
 
-        for pr in range(N // 2):
+        st = {}
+
+        def affinity(n):
+            mk_t, qk_t, mv_t, qv_t, i = place[n]
+            for u in range(2):
+                aff = ps_aff.tile([P, 2, Q], F32)
+                st[("aff", n, u)] = aff
+                for b in range(2):
+                    nc.tensor.matmul(
+                        out=aff[:, b, :],
+                        lhsT=mk_t[:, i, 256 * u + b:256 * (u + 1):2],
+                        rhs=qk_t[:, i, :],
+                        start=True,
+                        stop=True,
+                    )
+
+        def flip(pr):
             xt = ps_xt.tile([P, 2, 2, C], F32)
+            st[("xt", pr)] = xt
             for j in range(2):
                 mk_t, qk_t, mv_t, qv_t, i = place[2 * pr + j]
                 words = mv_t[:].bitcast(F32)
                 for u in range(2):
                     nc.tensor.transpose(xt[:, j, u, :], words[:, i, 128 * u:128 * (u + 1)], ident[:])
+
+        def flip_out(pr):
             vgrp = work.tile([P, 2, C, 4], BF16, align_bytes=64)
-            nc.scalar.copy(out=vgrp[:].bitcast(F32), in_=xt[:].rearrange("p j u c -> p j c u"))
+            st[("vgrp", pr)] = vgrp
+            nc.scalar.copy(out=vgrp[:].bitcast(F32), in_=st[("xt", pr)][:].rearrange("p j u c -> p j c u"))
+
+        def flip_quant(pr):
             nc.vector.quantize_mx(
                 out=vcodes[:, 2 * pr:2 * pr + 2, :].rearrange("p j c -> p (j c)").bitcast(FP8X4),
                 scales=vscales[:, 2 * pr:2 * pr + 2, :].rearrange("p j c -> p (j c)"),
-                in_=vgrp[:].rearrange("p j c t -> p (j c t)"),
+                in_=st[("vgrp", pr)][:].rearrange("p j c t -> p (j c t)"),
             )
 
-            res = work.tile([P, 2, 2, Q], F32)
-            mo = ps_mo.tile([P, 2, Q], F32)
-            for j in range(2):
-                n = 2 * pr + j
-                mk_t, qk_t, mv_t, qv_t, i = place[n]
+        def maxima(n, u):
+            if u == 0:
                 mx = small.tile([P, 4], F32)
-                nb = small.tile([P, 4], F32)
-                sums = small.tile([P, 4], F32)
-                rs = small.tile([P, 4], F32)
-                ex = work.tile([P, 4, Q], F32)
-                affs = []
-                for u in range(2):
-                    aff = ps_aff.tile([P, 2, Q], F32)
-                    for b in range(2):
-                        nc.tensor.matmul(
-                            out=aff[:, b, :],
-                            lhsT=mk_t[:, i, 256 * u + b:256 * (u + 1):2],
-                            rhs=qk_t[:, i, :],
-                            start=True,
-                            stop=True,
-                        )
-                    nc.vector.tensor_reduce(out=mx[:, 2 * u:2 * u + 2], in_=aff[:], axis=AX.X, op=ALU.max)
-                    affs.append(aff)
-                nc.scalar.mul(out=nb[:], in_=mx[:], mul=-SCALE)
-                for t in range(4):
-                    nc.scalar.activation(
-                        out=ex[:, t, :],
-                        in_=affs[t // 2][:, t % 2, :],
-                        func=ACT.Exp,
-                        bias=nb[:, t:t + 1],
-                        scale=SCALE,
-                        accum_out=sums[:, t:t + 1],
-                    )
-                nc.vector.reciprocal(out=rs[:], in_=sums[:])
-                grp = work.tile([P, Q, 4], BF16, align_bytes=64)
-                nc.vector.tensor_tensor(
-                    out=grp[:],
-                    in0=ex[:].rearrange("p t q -> p q t"),
-                    in1=rs[:].unsqueeze(1).to_broadcast([P, Q, 4]),
-                    op=ALU.mult,
+                st[("mx", n)] = mx
+            nc.vector.tensor_reduce(
+                out=st[("mx", n)][:, 2 * u:2 * u + 2], in_=st[("aff", n, u)][:], axis=AX.X, op=ALU.max
+            )
+
+        def exps(n):
+            nb = small.tile([P, 4], F32)
+            sums = small.tile([P, 4], F32)
+            ex = work.tile([P, 4, Q], F32)
+            st[("sums", n)] = sums
+            st[("ex", n)] = ex
+            nc.scalar.mul(out=nb[:], in_=st[("mx", n)][:], mul=-SCALE)
+            for t in range(4):
+                nc.scalar.activation(
+                    out=ex[:, t, :],
+                    in_=st[("aff", n, t // 2)][:, t % 2, :],
+                    func=ACT.Exp,
+                    bias=nb[:, t:t + 1],
+                    scale=SCALE,
+                    accum_out=sums[:, t:t + 1],
                 )
-                ac = work.tile([P, Q], U32, align_bytes=64)
-                asc = work.tile([P, Q], U8, align_bytes=64)
-                nc.vector.quantize_mx(
-                    out=ac[:].bitcast(FP8X4),
-                    scales=asc[:],
-                    in_=grp[:].rearrange("p q t -> p (q t)"),
-                )
-                nc.tensor.matmul_mx(
-                    out=mo[:, j, :],
-                    lhsT=vcodes[:, n, :].bitcast(FP8X4),
-                    lhsT_scale=vscales[:, n, :],
-                    rhs=ac[:].bitcast(FP8X4),
-                    rhs_scale=asc[:],
-                    start=True,
-                    stop=True,
-                )
-            mk_t, qk_t, mv_t, qv_t, i = place[2 * pr]
-            nc.scalar.copy(out=res[:, :, 1, :], in_=mo[:])
-            nc.scalar.copy(out=res[:, :, 0, :], in_=qv_t[:, i:i + 2, :])
+
+        def recip(n):
+            rs = small.tile([P, 4], F32)
+            st[("rs", n)] = rs
+            nc.vector.reciprocal(out=rs[:], in_=st[("sums", n)][:])
+
+        def normalise(eng, n, q0, q1):
+            grp = st[("grp", n)]
+            eng.tensor_tensor(
+                out=grp[:, q0:q1, :].rearrange("p (c i) t -> p c t i", i=RUN),
+                in0=st[("ex", n)][:, :, q0:q1].rearrange("p t (c i) -> p c t i", i=RUN),
+                in1=st[("rs", n)][:].unsqueeze(1).unsqueeze(3).to_broadcast([P, (q1 - q0) // RUN, 4, RUN]),
+                op=ALU.mult,
+            )
+
+        def quant(n):
+            ac = work.tile([P, Q], U32, align_bytes=64)
+            asc = work.tile([P, Q], U8, align_bytes=64)
+            st[("ac", n)] = (ac, asc)
+            nc.vector.quantize_mx(
+                out=ac[:].bitcast(FP8X4),
+                scales=asc[:],
+                in_=st[("grp", n)][:].rearrange("p q t -> p (q t)"),
+            )
+
+        def read_out(n):
+            if n % 2 == 0:
+                mo = ps_mo.tile([P, 2, Q], F32)
+                st[("mo", n // 2)] = mo
+            ac, asc = st[("ac", n)]
+            nc.tensor.matmul_mx(
+                out=st[("mo", n // 2)][:, n % 2, :],
+                lhsT=vcodes[:, n, :].bitcast(FP8X4),
+                lhsT_scale=vscales[:, n, :],
+                rhs=ac[:].bitcast(FP8X4),
+                rhs_scale=asc[:],
+                start=True,
+                stop=True,
+            )
+
+        def cast(n):
+            if n % 2 == 0:
+                res = work.tile([P, 2, 2, Q], F32)
+                st[("res", n // 2)] = res
+            mk_t, qk_t, mv_t, qv_t, i = place[n]
+            nc.scalar.copy(out=st[("res", n // 2)][:, n % 2, 0, :], in_=qv_t[:, i, :])
+
+        def finish(pr):
+            res = st[("res", pr)]
+            nc.scalar.copy(out=res[:, :, 1, :], in_=st[("mo", pr)][:])
             nc.sync.dma_start(out=out_d[:, 2 * pr:2 * pr + 2, :, :], in_=res[:])
+
+        later = list(range(FIRST, len(CHUNKS)))
+        for s in range(-3, N + 4):
+            if 0 <= s + 3 < N:
+                affinity(s + 3)
+            if (s + 3) % 2 == 0 and 0 <= (s + 3) // 2 < N // 2:
+                flip((s + 3) // 2)
+            if 0 <= s + 1 < N:
+                exps(s + 1)
+            if (s + 2) % 2 == 0 and 0 <= (s + 2) // 2 < N // 2:
+                flip_out((s + 2) // 2)
+            if 0 <= s - 2 < N:
+                cast(s - 2)
+            if (s - 3) % 2 == 0 and 0 <= (s - 3) // 2 < N // 2:
+                finish((s - 3) // 2)
+                if ((s - 3) // 2) % 2 == 0 and later:
+                    load(later.pop(0))
+            if 0 <= s < N:
+                grp = work.tile([P, Q, 4], BF16, align_bytes=64)
+                st[("grp", s)] = grp
+                if GQ:
+                    normalise(nc.gpsimd, s, Q - GQ, Q)
+            if 0 <= s + 2 < N:
+                maxima(s + 2, 0)
+                maxima(s + 2, 1)
+            if 0 <= s - 1 < N:
+                quant(s - 1)
+            if (s + 1) % 2 == 0 and 0 <= (s + 1) // 2 < N // 2:
+                flip_quant((s + 1) // 2)
+            if 0 <= s < N:
+                normalise(nc.vector, s, 0, Q - GQ)
+            if 0 <= s + 1 < N:
+                recip(s + 1)
+            if 0 <= s - 1 < N:
+                read_out(s - 1)

@@ -18,7 +18,7 @@ SCALE = 128 ** -0.5
 FLOPS = 2 * (2 * N * Q * M * C)
 CHUNKS = [2, 2, 4, 4, 4, 4, 4, 4, 4]
 FIRST = 4
-GQ = 0
+GQ = 96
 RUN = 4
 
 

@@ -16,10 +16,13 @@ N, C, Q, M = 32, 128, 256, 512
 P = 128
 SCALE = 128 ** -0.5
 FLOPS = 2 * (2 * N * Q * M * C)
-CHUNKS = [2, 2, 4, 4, 4, 4, 4, 4, 4]
-FIRST = 4
-GQ = 96
+CHUNKS = [1, 1, 2, 4, 4, 4, 4, 4, 4, 4]
+FIRST = 5
+HEAD_LOADS = [(0, ["mk", "qk"]), (1, ["mk", "qk"]), (0, ["mv"]), (1, ["mv"]), (2, ["mk", "qk", "mv"]), (0, ["qv"]), (1, ["qv"]), (2, ["qv"]), (3, ["mk", "qk", "mv", "qv"]), (4, ["mk", "qk", "mv", "qv"])]
+GQ = 128
+GQ_LAST = 0
 RUN = 4
+CAST_BY = 26
 
 
 def tile_stm_head_t_kernel(tc, q_key, q_val, m_key, m_val, out):
@@ -33,10 +36,12 @@ def tile_stm_head_t_kernel(tc, q_key, q_val, m_key, m_val, out):
     with ExitStack() as ctx:
         keep = ctx.enter_context(tc.tile_pool(name="keep", bufs=1))
         work = ctx.enter_context(tc.tile_pool(name="work", bufs=4))
+        outs = ctx.enter_context(tc.tile_pool(name="outs", bufs=6))
         small = ctx.enter_context(tc.tile_pool(name="small", bufs=6))
-        ps_aff = ctx.enter_context(tc.psum_pool(name="ps_aff", bufs=6))
+        ps_aff = ctx.enter_context(tc.psum_pool(name="ps_aff", bufs=5))
         ps_xt = ctx.enter_context(tc.psum_pool(name="ps_xt", bufs=1))
         ps_mo = ctx.enter_context(tc.psum_pool(name="ps_mo", bufs=1))
+        ps_rs = ctx.enter_context(tc.psum_pool(name="ps_rs", bufs=1))
         ctx.enter_context(tc.manual_schedule())
 
         ident = keep.tile([P, P], F32, name="ident")
@@ -44,30 +49,27 @@ def tile_stm_head_t_kernel(tc, q_key, q_val, m_key, m_val, out):
         vcodes = keep.tile([P, N, C], U32, name="vcodes", align_bytes=64)
         vscales = keep.tile([P, N, C], U8, name="vscales", align_bytes=64)
 
-        place = {}
         starts = [sum(CHUNKS[:ci]) for ci in range(len(CHUNKS))]
+        place = {}
 
-        def load(ci):
+        def load(ci, kinds):
             size = CHUNKS[ci]
             n0 = starts[ci]
-            mk_t = keep.tile([P, size, M], BF16, name="mk%d" % ci)
-            qk_t = keep.tile([P, size, Q], BF16, name="qk%d" % ci)
-            mv_t = keep.tile([P, size, M], BF16, name="mv%d" % ci)
-            qv_t = keep.tile([P, size, Q], BF16, name="qv%d" % ci)
-            nc.sync.dma_start(out=mk_t[:], in_=mk_d[:, n0:n0 + size, :])
-            nc.sync.dma_start(out=qk_t[:], in_=qk_d[:, n0:n0 + size, :])
-            nc.sync.dma_start(out=mv_t[:], in_=mv_d[:, n0:n0 + size, :])
-            nc.sync.dma_start(out=qv_t[:], in_=qv_d[:, n0:n0 + size, :])
-            for i in range(size):
-                place[n0 + i] = (mk_t, qk_t, mv_t, qv_t, i)
+            for kind in kinds:
+                src, width = {"mk": (mk_d, M), "qk": (qk_d, Q), "mv": (mv_d, M), "qv": (qv_d, Q)}[kind]
+                t = keep.tile([P, size, width], BF16, name="%s%d" % (kind, ci))
+                nc.sync.dma_start(out=t[:], in_=src[:, n0:n0 + size, :])
+                for i in range(size):
+                    place[(kind, n0 + i)] = (t, i)
 
-        for ci in range(FIRST):
-            load(ci)
+        for ci, kinds in HEAD_LOADS:
+            load(ci, kinds)
 
         st = {}
 
         def affinity(n):
-            mk_t, qk_t, mv_t, qv_t, i = place[n]
+            mk_t, i = place[("mk", n)]
+            qk_t, i = place[("qk", n)]
             for u in range(2):
                 aff = ps_aff.tile([P, 2, Q], F32)
                 st[("aff", n, u)] = aff
@@ -84,7 +86,7 @@ def tile_stm_head_t_kernel(tc, q_key, q_val, m_key, m_val, out):
             xt = ps_xt.tile([P, 2, 2, C], F32)
             st[("xt", pr)] = xt
             for j in range(2):
-                mk_t, qk_t, mv_t, qv_t, i = place[2 * pr + j]
+                mv_t, i = place[("mv", 2 * pr + j)]
                 words = mv_t[:].bitcast(F32)
                 for u in range(2):
                     nc.tensor.transpose(xt[:, j, u, :], words[:, i, 128 * u:128 * (u + 1)], ident[:])
@@ -94,11 +96,11 @@ def tile_stm_head_t_kernel(tc, q_key, q_val, m_key, m_val, out):
             st[("vgrp", pr)] = vgrp
             nc.scalar.copy(out=vgrp[:].bitcast(F32), in_=st[("xt", pr)][:].rearrange("p j u c -> p j c u"))
 
-        def flip_quant(pr):
+        def flip_quant(n):
             nc.vector.quantize_mx(
-                out=vcodes[:, 2 * pr:2 * pr + 2, :].rearrange("p j c -> p (j c)").bitcast(FP8X4),
-                scales=vscales[:, 2 * pr:2 * pr + 2, :].rearrange("p j c -> p (j c)"),
-                in_=st[("vgrp", pr)][:].rearrange("p j c t -> p (j c t)"),
+                out=vcodes[:, n, :].bitcast(FP8X4),
+                scales=vscales[:, n, :],
+                in_=st[("vgrp", n // 2)][:, n % 2, :, :].rearrange("p c t -> p (c t)"),
             )
 
         def maxima(n, u):
@@ -109,13 +111,17 @@ def tile_stm_head_t_kernel(tc, q_key, q_val, m_key, m_val, out):
                 out=st[("mx", n)][:, 2 * u:2 * u + 2], in_=st[("aff", n, u)][:], axis=AX.X, op=ALU.max
             )
 
-        def exps(n):
+        def shift(n):
             nb = small.tile([P, 4], F32)
+            st[("nb", n)] = nb
+            nc.vector.tensor_scalar(out=nb[:], in0=st[("mx", n)][:], scalar1=-SCALE, scalar2=None, op0=ALU.mult)
+
+        def exps(n):
             sums = small.tile([P, 4], F32)
             ex = work.tile([P, 4, Q], F32)
             st[("sums", n)] = sums
             st[("ex", n)] = ex
-            nc.scalar.mul(out=nb[:], in_=st[("mx", n)][:], mul=-SCALE)
+            nb = st[("nb", n)]
             for t in range(4):
                 nc.scalar.activation(
                     out=ex[:, t, :],
@@ -130,13 +136,19 @@ def tile_stm_head_t_kernel(tc, q_key, q_val, m_key, m_val, out):
             rs = small.tile([P, 4], F32)
             st[("rs", n)] = rs
             nc.vector.reciprocal(out=rs[:], in_=st[("sums", n)][:])
+            if share(n):
+                rsp = ps_rs.tile([P, 4], F32)
+                st[("rsp", n)] = rsp
+                nc.tensor.matmul(out=rsp[:], lhsT=ident[:], rhs=rs[:], start=True, stop=True)
+            else:
+                st[("rsp", n)] = rs
 
-        def normalise(eng, n, q0, q1):
+        def normalise(eng, n, q0, q1, factor):
             grp = st[("grp", n)]
             eng.tensor_tensor(
                 out=grp[:, q0:q1, :].rearrange("p (c i) t -> p c t i", i=RUN),
                 in0=st[("ex", n)][:, :, q0:q1].rearrange("p t (c i) -> p c t i", i=RUN),
-                in1=st[("rs", n)][:].unsqueeze(1).unsqueeze(3).to_broadcast([P, (q1 - q0) // RUN, 4, RUN]),
+                in1=factor[:].unsqueeze(1).unsqueeze(3).to_broadcast([P, (q1 - q0) // RUN, 4, RUN]),
                 op=ALU.mult,
             )
 
@@ -167,9 +179,9 @@ def tile_stm_head_t_kernel(tc, q_key, q_val, m_key, m_val, out):
 
         def cast(n):
             if n % 2 == 0:
-                res = work.tile([P, 2, 2, Q], F32)
+                res = outs.tile([P, 2, 2, Q], F32)
                 st[("res", n // 2)] = res
-            mk_t, qk_t, mv_t, qv_t, i = place[n]
+            qv_t, i = place[("qv", n)]
             nc.scalar.copy(out=st[("res", n // 2)][:, n % 2, 0, :], in_=qv_t[:, i, :])
 
         def finish(pr):
@@ -177,37 +189,62 @@ def tile_stm_head_t_kernel(tc, q_key, q_val, m_key, m_val, out):
             nc.scalar.copy(out=res[:, :, 1, :], in_=st[("mo", pr)][:])
             nc.sync.dma_start(out=out_d[:, 2 * pr:2 * pr + 2, :, :], in_=res[:])
 
+        def finish_one(n):
+            res = st[("res", n // 2)]
+            nc.scalar.copy(out=res[:, n % 2, 1, :], in_=st[("mo", n // 2)][:, n % 2, :])
+            nc.sync.dma_start(out=out_d[:, n, 1, :], in_=res[:, n % 2, 1, :])
+
+        def share(n):
+            return GQ_LAST if n >= N - 2 else GQ
+
         later = list(range(FIRST, len(CHUNKS)))
-        for s in range(-3, N + 4):
-            if 0 <= s + 3 < N:
-                affinity(s + 3)
-            if (s + 3) % 2 == 0 and 0 <= (s + 3) // 2 < N // 2:
-                flip((s + 3) // 2)
-            if 0 <= s + 1 < N:
-                exps(s + 1)
-            if (s + 2) % 2 == 0 and 0 <= (s + 2) // 2 < N // 2:
-                flip_out((s + 2) // 2)
-            if 0 <= s - 2 < N:
-                cast(s - 2)
-            if (s - 3) % 2 == 0 and 0 <= (s - 3) // 2 < N // 2:
-                finish((s - 3) // 2)
-                if ((s - 3) // 2) % 2 == 0 and later:
-                    load(later.pop(0))
+        casts = [0]
+        LASTP = N // 2 - 1
+        for s in range(-3, N + 2):
             if 0 <= s < N:
+                recip(s)
                 grp = work.tile([P, Q, 4], BF16, align_bytes=64)
                 st[("grp", s)] = grp
-                if GQ:
-                    normalise(nc.gpsimd, s, Q - GQ, Q)
+                if share(s):
+                    normalise(nc.gpsimd, s, Q - share(s), Q, st[("rs", s)])
+            if 0 <= s - 1 < N:
+                read_out(s - 1)
+            if 0 <= s + 3 < N:
+                affinity(s + 3)
+            if 0 <= s + 1 < N:
+                exps(s + 1)
+            if s == -1:
+                flip_out(0)
+            if (s + 2) % 2 == 0 and 1 <= (s + 2) // 2 < N // 2:
+                flip_out((s + 2) // 2)
+            want = min(N, ((s + 2) * N + CAST_BY + 1) // (CAST_BY + 2)) if s >= -1 else 0
+            while casts[0] < want:
+                cast(casts[0])
+                if casts[0] == N - 1:
+                    nc.sync.dma_start(out=out_d[:, N - 2:N, 0, :], in_=st[("res", LASTP)][:, :, 0, :])
+                casts[0] += 1
+            if (s - 2) % 2 == 0 and 0 <= (s - 2) // 2 < LASTP:
+                finish((s - 2) // 2)
+                if ((s - 2) // 2) % 2 == 0 and later:
+                    load(later.pop(0), ["mk", "qk", "mv", "qv"])
+            if s == N:
+                finish_one(N - 2)
+            if s == N + 1:
+                finish_one(N - 1)
+            if s == -2:
+                flip(0)
+            if (s + 3) % 2 == 0 and 1 <= (s + 3) // 2 < N // 2:
+                flip((s + 3) // 2)
             if 0 <= s + 2 < N:
                 maxima(s + 2, 0)
                 maxima(s + 2, 1)
-            if 0 <= s - 1 < N:
-                quant(s - 1)
-            if (s + 1) % 2 == 0 and 0 <= (s + 1) // 2 < N // 2:
-                flip_quant((s + 1) // 2)
             if 0 <= s < N:
-                normalise(nc.vector, s, 0, Q - GQ)
-            if 0 <= s + 1 < N:
-                recip(s + 1)
-            if 0 <= s - 1 < N:
-                read_out(s - 1)
+                normalise(nc.vector, s, 0, Q - share(s), st[("rsp", s)])
+            if 0 <= s + 2 < N:
+                shift(s + 2)
+            if s == 0:
+                flip_quant(0)
+            if 0 <= s and s + 1 < N:
+                flip_quant(s + 1)
+            if 0 <= s < N:
+                quant(s)

@@ -18,11 +18,12 @@ SCALE = 128 ** -0.5
 FLOPS = 2 * (2 * N * Q * M * C)
 CHUNKS = [1, 1, 2, 4, 4, 4, 4, 4, 4, 4]
 FIRST = 5
-HEAD_LOADS = [(0, ["mk", "qk"]), (1, ["mk", "qk"]), (0, ["mv"]), (1, ["mv"]), (2, ["mk", "qk", "mv"]), (0, ["qv"]), (1, ["qv"]), (2, ["qv"]), (3, ["mk", "qk", "mv", "qv"]), (4, ["mk", "qk", "mv", "qv"])]
-GQ = 128
+HEAD_LOADS = [(0, ["mk", "qk"]), (0, ["mv"]), (1, ["mv"]), (1, ["mk", "qk"]), (-1, 0), (2, ["mk", "qk", "mv"]), (3, ["mk", "qk", "mv"]), (-1, 1), (4, ["mk", "qk", "mv"]), (-1, 2)]
+GQ = 144
 GQ_LAST = 0
 RUN = 4
-CAST_BY = 26
+QC = 4
+CASTS = {3: [2], 5: [3], 8: [4], 10: [5], 12: [6], 14: [7], 17: [8], 19: [9], 21: [10], 23: [11], 26: [12], 28: [13], 31: [14], 32: [15]}
 
 
 def tile_stm_head_t_kernel(tc, q_key, q_val, m_key, m_val, out):
@@ -36,13 +37,18 @@ def tile_stm_head_t_kernel(tc, q_key, q_val, m_key, m_val, out):
     with ExitStack() as ctx:
         keep = ctx.enter_context(tc.tile_pool(name="keep", bufs=1))
         work = ctx.enter_context(tc.tile_pool(name="work", bufs=4))
-        outs = ctx.enter_context(tc.tile_pool(name="outs", bufs=6))
+        outs = ctx.enter_context(tc.tile_pool(name="outs", bufs=4))
         small = ctx.enter_context(tc.tile_pool(name="small", bufs=6))
         ps_aff = ctx.enter_context(tc.psum_pool(name="ps_aff", bufs=5))
         ps_xt = ctx.enter_context(tc.psum_pool(name="ps_xt", bufs=1))
         ps_mo = ctx.enter_context(tc.psum_pool(name="ps_mo", bufs=1))
         ps_rs = ctx.enter_context(tc.psum_pool(name="ps_rs", bufs=1))
         ctx.enter_context(tc.manual_schedule())
+
+        zero = keep.tile([P, 1], F32, name="zero")
+        one = keep.tile([P, 1], F32, name="one")
+        nc.vector.memset(zero[:], 0.0)
+        nc.scalar.activation(out=one[:], in_=zero[:], func=ACT.Exp)
 
         ident = keep.tile([P, P], F32, name="ident")
         make_identity(nc, ident[:])
@@ -62,8 +68,17 @@ def tile_stm_head_t_kernel(tc, q_key, q_val, m_key, m_val, out):
                 for i in range(size):
                     place[(kind, n0 + i)] = (t, i)
 
+        def load_qv(j):
+            t = keep.tile([P, QC, Q], BF16, name="qv%d" % j)
+            nc.sync.dma_start(out=t[:], in_=qv_d[:, QC * j:QC * (j + 1), :])
+            for i in range(QC):
+                place[("qv", QC * j + i)] = (t, i)
+
         for ci, kinds in HEAD_LOADS:
-            load(ci, kinds)
+            if ci < 0:
+                load_qv(kinds)
+            else:
+                load(ci, kinds)
 
         st = {}
 
@@ -177,32 +192,38 @@ def tile_stm_head_t_kernel(tc, q_key, q_val, m_key, m_val, out):
                 stop=True,
             )
 
-        def cast(n):
-            if n % 2 == 0:
-                res = outs.tile([P, 2, 2, Q], F32)
-                st[("res", n // 2)] = res
-            qv_t, i = place[("qv", n)]
-            nc.scalar.copy(out=st[("res", n // 2)][:, n % 2, 0, :], in_=qv_t[:, i, :])
+        def cast_head():
+            qv_t, i = place[("qv", 0)]
+            qf4 = keep.tile([P, QC, Q], F32, name="qf4")
+            nc.gpsimd.tensor_scalar(out=qf4[:], in0=qv_t[:], scalar1=1.0, scalar2=0.0, op0=ALU.mult, op1=ALU.add)
+            nc.sync.dma_start(out=out_d[:, 0:QC, 0, :], in_=qf4[:])
+
+        def cast(pr):
+            qv_t, i = place[("qv", 2 * pr)]
+            qf = outs.tile([P, 2, Q], F32)
+            nc.scalar.copy(out=qf[:], in_=qv_t[:, i:i + 2, :])
+            nc.sync.dma_start(out=out_d[:, 2 * pr:2 * pr + 2, 0, :], in_=qf[:])
 
         def finish(pr):
-            res = st[("res", pr)]
-            nc.scalar.copy(out=res[:, :, 1, :], in_=st[("mo", pr)][:])
-            nc.sync.dma_start(out=out_d[:, 2 * pr:2 * pr + 2, :, :], in_=res[:])
+            res = outs.tile([P, 2, Q], F32)
+            nc.scalar.copy(out=res[:], in_=st[("mo", pr)][:])
+            nc.sync.dma_start(out=out_d[:, 2 * pr:2 * pr + 2, 1, :], in_=res[:])
 
         def finish_one(n):
-            res = st[("res", n // 2)]
-            nc.scalar.copy(out=res[:, n % 2, 1, :], in_=st[("mo", n // 2)][:, n % 2, :])
-            nc.sync.dma_start(out=out_d[:, n, 1, :], in_=res[:, n % 2, 1, :])
+            last = outs.tile([P, Q], F32)
+            nc.scalar.copy(out=last[:], in_=st[("mo", n // 2)][:, n % 2, :])
+            nc.sync.dma_start(out=out_d[:, n, 1, :], in_=last[:])
 
         def share(n):
             return GQ_LAST if n >= N - 2 else GQ
 
         later = list(range(FIRST, len(CHUNKS)))
-        casts = [0]
         LASTP = N // 2 - 1
+        cast_head()
         for s in range(-3, N + 2):
             if 0 <= s < N:
-                recip(s)
+                if share(s):
+                    recip(s)
                 grp = work.tile([P, Q, 4], BF16, align_bytes=64)
                 st[("grp", s)] = grp
                 if share(s):
@@ -211,27 +232,25 @@ def tile_stm_head_t_kernel(tc, q_key, q_val, m_key, m_val, out):
                 read_out(s - 1)
             if 0 <= s + 3 < N:
                 affinity(s + 3)
+            if s == -2:
+                flip_out(0)
             if 0 <= s + 1 < N:
                 exps(s + 1)
-            if s == -1:
-                flip_out(0)
             if (s + 2) % 2 == 0 and 1 <= (s + 2) // 2 < N // 2:
                 flip_out((s + 2) // 2)
-            want = min(N, ((s + 2) * N + CAST_BY + 1) // (CAST_BY + 2)) if s >= -1 else 0
-            while casts[0] < want:
-                cast(casts[0])
-                if casts[0] == N - 1:
-                    nc.sync.dma_start(out=out_d[:, N - 2:N, 0, :], in_=st[("res", LASTP)][:, :, 0, :])
-                casts[0] += 1
             if (s - 2) % 2 == 0 and 0 <= (s - 2) // 2 < LASTP:
                 finish((s - 2) // 2)
                 if ((s - 2) // 2) % 2 == 0 and later:
-                    load(later.pop(0), ["mk", "qk", "mv", "qv"])
+                    ci = later.pop(0)
+                    load(ci, ["mk", "qk", "mv"])
+                    load_qv(ci - 2)
             if s == N:
                 finish_one(N - 2)
+            for pr in CASTS.get(s, []):
+                cast(pr)
             if s == N + 1:
                 finish_one(N - 1)
-            if s == -2:
+            if s == -3:
                 flip(0)
             if (s + 3) % 2 == 0 and 1 <= (s + 3) // 2 < N // 2:
                 flip((s + 3) // 2)
@@ -242,6 +261,8 @@ def tile_stm_head_t_kernel(tc, q_key, q_val, m_key, m_val, out):
                 normalise(nc.vector, s, 0, Q - share(s), st[("rsp", s)])
             if 0 <= s + 2 < N:
                 shift(s + 2)
+            if 0 <= s + 1 < N and not share(s + 1):
+                recip(s + 1)
             if s == 0:
                 flip_quant(0)
             if 0 <= s and s + 1 < N:

@@ -22,6 +22,8 @@ HEAD_LOADS = [(0, ["mk", "qk"]), (0, ["mv"]), (1, ["mv"]), (1, ["mk", "qk"]), (-
 GQ = 144
 GQ_LAST = 0
 RUN = 4
+PAD = 80
+RING = 6
 QC = 4
 CASTS = {3: [2], 5: [3], 8: [4], 10: [5], 12: [6], 14: [7], 17: [8], 19: [9], 21: [10], 23: [11], 26: [12], 28: [13], 31: [14], 32: [15]}
 
@@ -52,6 +54,8 @@ def tile_stm_head_t_kernel(tc, q_key, q_val, m_key, m_val, out):
 
         ident = keep.tile([P, P], F32, name="ident")
         make_identity(nc, ident[:])
+        rsw = keep.tile([P, RING, PAD], F32, name="rsw")
+        nc.vector.memset(rsw[:], 0.0)
         vcodes = keep.tile([P, N, C], U32, name="vcodes", align_bytes=64)
         vscales = keep.tile([P, N, C], U8, name="vscales", align_bytes=64)
 
@@ -148,13 +152,13 @@ def tile_stm_head_t_kernel(tc, q_key, q_val, m_key, m_val, out):
                 )
 
         def recip(n):
-            rs = small.tile([P, 4], F32)
+            rs = rsw[:, n % RING, 0:4]
             st[("rs", n)] = rs
-            nc.vector.reciprocal(out=rs[:], in_=st[("sums", n)][:])
+            nc.vector.reciprocal(out=rs, in_=st[("sums", n)][:])
             if share(n):
-                rsp = ps_rs.tile([P, 4], F32)
-                st[("rsp", n)] = rsp
-                nc.tensor.matmul(out=rsp[:], lhsT=ident[:], rhs=rs[:], start=True, stop=True)
+                rsp = ps_rs.tile([P, PAD], F32)
+                st[("rsp", n)] = rsp[:, 0:4]
+                nc.tensor.matmul(out=rsp[:], lhsT=ident[:], rhs=rsw[:, n % RING, :], start=True, stop=True)
             else:
                 st[("rsp", n)] = rs
 
@@ -163,7 +167,7 @@ def tile_stm_head_t_kernel(tc, q_key, q_val, m_key, m_val, out):
             eng.tensor_tensor(
                 out=grp[:, q0:q1, :].rearrange("p (c i) t -> p c t i", i=RUN),
                 in0=st[("ex", n)][:, :, q0:q1].rearrange("p t (c i) -> p c t i", i=RUN),
-                in1=factor[:].unsqueeze(1).unsqueeze(3).to_broadcast([P, (q1 - q0) // RUN, 4, RUN]),
+                in1=factor.unsqueeze(1).unsqueeze(3).to_broadcast([P, (q1 - q0) // RUN, 4, RUN]),
                 op=ALU.mult,
             )
 

@@ -19,13 +19,14 @@ FLOPS = 2 * (2 * N * Q * M * C)
 CHUNKS = [1, 1, 2, 4, 4, 4, 4, 4, 4, 4]
 FIRST = 5
 HEAD_LOADS = [(0, ["mk", "qk"]), (0, ["mv"]), (1, ["mv"]), (1, ["mk", "qk"]), (-1, 0), (2, ["mk", "qk", "mv"]), (3, ["mk", "qk", "mv"]), (-1, 1), (4, ["mk", "qk", "mv"]), (-1, 2)]
-GQ = 144
+GQ = 152
 GQ_LAST = 0
 RUN = 4
 PAD = 80
 RING = 6
 QC = 4
-CASTS = {3: [2], 5: [3], 8: [4], 10: [5], 12: [6], 14: [7], 17: [8], 19: [9], 21: [10], 23: [11], 26: [12], 28: [13], 31: [14], 32: [15]}
+CASTS = {3: [2], 5: [3], 10: [5], 12: [6], 17: [8], 19: [9], 23: [11], 26: [12], 31: [14], 32: [15]}
+VCASTS = {8: [4], 14: [7], 21: [10], 28: [13]}
 
 
 def tile_stm_head_t_kernel(tc, q_key, q_val, m_key, m_val, out):
@@ -202,10 +203,13 @@ def tile_stm_head_t_kernel(tc, q_key, q_val, m_key, m_val, out):
             nc.gpsimd.tensor_scalar(out=qf4[:], in0=qv_t[:], scalar1=1.0, scalar2=0.0, op0=ALU.mult, op1=ALU.add)
             nc.sync.dma_start(out=out_d[:, 0:QC, 0, :], in_=qf4[:])
 
-        def cast(pr):
+        def cast(pr, on_vector=False):
             qv_t, i = place[("qv", 2 * pr)]
             qf = outs.tile([P, 2, Q], F32)
-            nc.scalar.copy(out=qf[:], in_=qv_t[:, i:i + 2, :])
+            if on_vector:
+                nc.vector.tensor_copy(out=qf[:], in_=qv_t[:, i:i + 2, :])
+            else:
+                nc.scalar.copy(out=qf[:], in_=qv_t[:, i:i + 2, :])
             nc.sync.dma_start(out=out_d[:, 2 * pr:2 * pr + 2, 0, :], in_=qf[:])
 
         def finish(pr):
@@ -225,13 +229,6 @@ def tile_stm_head_t_kernel(tc, q_key, q_val, m_key, m_val, out):
         LASTP = N // 2 - 1
         cast_head()
         for s in range(-3, N + 2):
-            if 0 <= s < N:
-                if share(s):
-                    recip(s)
-                grp = work.tile([P, Q, 4], BF16, align_bytes=64)
-                st[("grp", s)] = grp
-                if share(s):
-                    normalise(nc.gpsimd, s, Q - share(s), Q, st[("rs", s)])
             if 0 <= s - 1 < N:
                 read_out(s - 1)
             if 0 <= s + 3 < N:
@@ -265,11 +262,18 @@ def tile_stm_head_t_kernel(tc, q_key, q_val, m_key, m_val, out):
                 normalise(nc.vector, s, 0, Q - share(s), st[("rsp", s)])
             if 0 <= s + 2 < N:
                 shift(s + 2)
-            if 0 <= s + 1 < N and not share(s + 1):
-                recip(s + 1)
             if s == 0:
                 flip_quant(0)
             if 0 <= s and s + 1 < N:
                 flip_quant(s + 1)
+            if 0 <= s + 1 < N:
+                recip(s + 1)
             if 0 <= s < N:
                 quant(s)
+            for pr in VCASTS.get(s, []):
+                cast(pr, True)
+            if 0 <= s + 1 < N:
+                grp = work.tile([P, Q, 4], BF16, align_bytes=64)
+                st[("grp", s + 1)] = grp
+                if share(s + 1):
+                    normalise(nc.gpsimd, s + 1, Q - share(s + 1), Q, st[("rs", s + 1)])

@@ -18,15 +18,16 @@ SCALE = 128 ** -0.5
 FLOPS = 2 * (2 * N * Q * M * C)
 CHUNKS = [1, 1, 2, 4, 4, 4, 4, 4, 4, 4]
 FIRST = 5
-HEAD_LOADS = [(0, ["mk", "qk"]), (0, ["mv"]), (1, ["mv"]), (1, ["mk", "qk"]), (-1, 0), (2, ["mk", "qk", "mv"]), (3, ["mk", "qk", "mv"]), (-1, 1), (4, ["mk", "qk", "mv"]), (-1, 2)]
-GQ = 152
+HEAD_LOADS = [(0, ["mk", "qk"]), (0, ["mv"]), (1, ["mk", "qk"]), (1, ["mv"]), (-1, 0), (2, ["mk", "qk", "mv"]), (3, ["mk", "qk", "mv"]), (-1, 1), (4, ["mk", "qk", "mv"]), (-1, 2)]
+GROUPS = [[0]] + [[n, n + 1] for n in range(1, N - 1, 2)] + [[N - 1]]
+LAST = len(GROUPS) - 1
+GQ = 160
 GQ_LAST = 0
 RUN = 4
 PAD = 80
-RING = 6
+RING = 4
 QC = 4
-CASTS = {3: [2], 5: [3], 10: [5], 12: [6], 17: [8], 19: [9], 23: [11], 26: [12], 31: [14], 32: [15]}
-VCASTS = {8: [4], 14: [7], 21: [10], 28: [13]}
+V_CASTS = [1, 3, 5, 7, 9, 11, 13]
 
 
 def tile_stm_head_t_kernel(tc, q_key, q_val, m_key, m_val, out):
@@ -39,7 +40,7 @@ def tile_stm_head_t_kernel(tc, q_key, q_val, m_key, m_val, out):
 
     with ExitStack() as ctx:
         keep = ctx.enter_context(tc.tile_pool(name="keep", bufs=1))
-        work = ctx.enter_context(tc.tile_pool(name="work", bufs=4))
+        work = ctx.enter_context(tc.tile_pool(name="work", bufs=3))
         outs = ctx.enter_context(tc.tile_pool(name="outs", bufs=4))
         small = ctx.enter_context(tc.tile_pool(name="small", bufs=6))
         ps_aff = ctx.enter_context(tc.psum_pool(name="ps_aff", bufs=5))
@@ -55,8 +56,10 @@ def tile_stm_head_t_kernel(tc, q_key, q_val, m_key, m_val, out):
 
         ident = keep.tile([P, P], F32, name="ident")
         make_identity(nc, ident[:])
-        rsw = keep.tile([P, RING, PAD], F32, name="rsw")
+        rsw = keep.tile([P, RING, 2, PAD], F32, name="rsw")
         nc.vector.memset(rsw[:], 0.0)
+        mxs = keep.tile([P, RING, 4, 2], F32, name="mxs")
+        nc.vector.memset(mxs[:], -SCALE)
         vcodes = keep.tile([P, N, C], U32, name="vcodes", align_bytes=64)
         vscales = keep.tile([P, N, C], U8, name="vscales", align_bytes=64)
 
@@ -67,7 +70,7 @@ def tile_stm_head_t_kernel(tc, q_key, q_val, m_key, m_val, out):
             size = CHUNKS[ci]
             n0 = starts[ci]
             for kind in kinds:
-                src, width = {"mk": (mk_d, M), "qk": (qk_d, Q), "mv": (mv_d, M), "qv": (qv_d, Q)}[kind]
+                src, width = {"mk": (mk_d, M), "qk": (qk_d, Q), "mv": (mv_d, M)}[kind]
                 t = keep.tile([P, size, width], BF16, name="%s%d" % (kind, ci))
                 nc.sync.dma_start(out=t[:], in_=src[:, n0:n0 + size, :])
                 for i in range(size):
@@ -87,115 +90,137 @@ def tile_stm_head_t_kernel(tc, q_key, q_val, m_key, m_val, out):
 
         st = {}
 
-        def affinity(n):
+        def share(g):
+            return GQ_LAST if g >= LAST else GQ
+
+        def affinity(n, u):
             mk_t, i = place[("mk", n)]
             qk_t, i = place[("qk", n)]
-            for u in range(2):
-                aff = ps_aff.tile([P, 2, Q], F32)
-                st[("aff", n, u)] = aff
-                for b in range(2):
-                    nc.tensor.matmul(
-                        out=aff[:, b, :],
-                        lhsT=mk_t[:, i, 256 * u + b:256 * (u + 1):2],
-                        rhs=qk_t[:, i, :],
-                        start=True,
-                        stop=True,
-                    )
+            aff = ps_aff.tile([P, 2, Q], F32)
+            st[("aff", n, u)] = aff
+            for b in range(2):
+                nc.tensor.matmul(
+                    out=aff[:, b, :],
+                    lhsT=mk_t[:, i, 256 * u + b:256 * (u + 1):2],
+                    rhs=qk_t[:, i, :],
+                    start=True,
+                    stop=True,
+                )
 
-        def flip(pr):
+        def flip(g):
             xt = ps_xt.tile([P, 2, 2, C], F32)
-            st[("xt", pr)] = xt
-            for j in range(2):
-                mv_t, i = place[("mv", 2 * pr + j)]
+            st[("xt", g)] = xt
+            for j in range(len(GROUPS[g])):
+                mv_t, i = place[("mv", GROUPS[g][j])]
                 words = mv_t[:].bitcast(F32)
                 for u in range(2):
                     nc.tensor.transpose(xt[:, j, u, :], words[:, i, 128 * u:128 * (u + 1)], ident[:])
 
-        def flip_out(pr):
+        def flip_out(g):
+            k = len(GROUPS[g])
             vgrp = work.tile([P, 2, C, 4], BF16, align_bytes=64)
-            st[("vgrp", pr)] = vgrp
-            nc.scalar.copy(out=vgrp[:].bitcast(F32), in_=st[("xt", pr)][:].rearrange("p j u c -> p j c u"))
+            st[("vgrp", g)] = vgrp
+            nc.scalar.copy(
+                out=vgrp[:, 0:k].bitcast(F32), in_=st[("xt", g)][:, 0:k].rearrange("p j u c -> p j c u")
+            )
 
-        def flip_quant(n):
+        def flip_quant(g):
+            k = len(GROUPS[g])
+            n = GROUPS[g][0]
             nc.vector.quantize_mx(
-                out=vcodes[:, n, :].bitcast(FP8X4),
-                scales=vscales[:, n, :],
-                in_=st[("vgrp", n // 2)][:, n % 2, :, :].rearrange("p c t -> p (c t)"),
+                out=vcodes[:, n:n + k, :].rearrange("p j c -> p (j c)").bitcast(FP8X4),
+                scales=vscales[:, n:n + k, :].rearrange("p j c -> p (j c)"),
+                in_=st[("vgrp", g)][:, 0:k].rearrange("p j c t -> p (j c t)"),
             )
 
-        def maxima(n, u):
-            if u == 0:
-                mx = small.tile([P, 4], F32)
-                st[("mx", n)] = mx
-            nc.vector.tensor_reduce(
-                out=st[("mx", n)][:, 2 * u:2 * u + 2], in_=st[("aff", n, u)][:], axis=AX.X, op=ALU.max
-            )
+        def maxima(n):
+            for u in range(2):
+                nc.vector.tensor_reduce(
+                    out=mxs[:, n % RING, 2 * u:2 * u + 2, 0], in_=st[("aff", n, u)][:], axis=AX.X, op=ALU.max
+                )
 
         def shift(n):
             nb = small.tile([P, 4], F32)
             st[("nb", n)] = nb
-            nc.vector.tensor_scalar(out=nb[:], in0=st[("mx", n)][:], scalar1=-SCALE, scalar2=None, op0=ALU.mult)
+            nc.vector.tensor_reduce(out=nb[:], in_=mxs[:, n % RING], axis=AX.X, op=ALU.mult)
 
-        def exps(n):
-            sums = small.tile([P, 4], F32)
-            ex = work.tile([P, 4, Q], F32)
-            st[("sums", n)] = sums
-            st[("ex", n)] = ex
+        def exps(g, j):
+            n = GROUPS[g][j]
+            if j == 0:
+                sums = small.tile([P, 2, 4], F32)
+                ex = work.tile([P, 2, 4, Q], F32)
+                st[("sums", g)] = sums
+                st[("ex", g)] = ex
             nb = st[("nb", n)]
             for t in range(4):
                 nc.scalar.activation(
-                    out=ex[:, t, :],
+                    out=st[("ex", g)][:, j, t, :],
                     in_=st[("aff", n, t // 2)][:, t % 2, :],
                     func=ACT.Exp,
                     bias=nb[:, t:t + 1],
                     scale=SCALE,
-                    accum_out=sums[:, t:t + 1],
+                    accum_out=st[("sums", g)][:, j, t:t + 1],
                 )
 
-        def recip(n):
-            rs = rsw[:, n % RING, 0:4]
-            st[("rs", n)] = rs
-            nc.vector.reciprocal(out=rs, in_=st[("sums", n)][:])
-            if share(n):
-                rsp = ps_rs.tile([P, PAD], F32)
-                st[("rsp", n)] = rsp[:, 0:4]
-                nc.tensor.matmul(out=rsp[:], lhsT=ident[:], rhs=rsw[:, n % RING, :], start=True, stop=True)
-            else:
-                st[("rsp", n)] = rs
+        def recip(g):
+            k = len(GROUPS[g])
+            nc.vector.reciprocal(out=rsw[:, g % RING, 0:k, 0:4], in_=st[("sums", g)][:, 0:k, :])
 
-        def normalise(eng, n, q0, q1, factor):
-            grp = st[("grp", n)]
+        def spread(g, j):
+            if share(g):
+                if j == 0:
+                    rsp = ps_rs.tile([P, 2, PAD], F32)
+                    st[("rsp", g)] = rsp
+                nc.tensor.matmul(
+                    out=st[("rsp", g)][:, j, :], lhsT=ident[:], rhs=rsw[:, g % RING, j, :], start=True, stop=True
+                )
+
+        def new_grp(g):
+            grp = work.tile([P, 2, Q, 4], BF16, align_bytes=64)
+            st[("grp", g)] = grp
+
+        def normalise(eng, g, j, q0, q1, factor):
             eng.tensor_tensor(
-                out=grp[:, q0:q1, :].rearrange("p (c i) t -> p c t i", i=RUN),
-                in0=st[("ex", n)][:, :, q0:q1].rearrange("p t (c i) -> p c t i", i=RUN),
-                in1=factor.unsqueeze(1).unsqueeze(3).to_broadcast([P, (q1 - q0) // RUN, 4, RUN]),
+                out=st[("grp", g)][:, j, q0:q1, :].rearrange("p (c i) t -> p c t i", i=RUN),
+                in0=st[("ex", g)][:, j, :, q0:q1].rearrange("p t (c i) -> p c t i", i=RUN),
+                in1=factor[:, j, 0:4].unsqueeze(1).unsqueeze(3).to_broadcast([P, (q1 - q0) // RUN, 4, RUN]),
                 op=ALU.mult,
             )
 
-        def quant(n):
-            ac = work.tile([P, Q], U32, align_bytes=64)
-            asc = work.tile([P, Q], U8, align_bytes=64)
-            st[("ac", n)] = (ac, asc)
+        def vector_share(g, j):
+            factor = st[("rsp", g)] if share(g) else rsw[:, g % RING]
+            normalise(nc.vector, g, j, 0, Q - share(g), factor)
+
+        def gpsimd_share(g, j):
+            if share(g):
+                normalise(nc.gpsimd, g, j, Q - share(g), Q, rsw[:, g % RING])
+
+        def quant(g):
+            k = len(GROUPS[g])
+            ac = work.tile([P, 2, Q], U32, align_bytes=64)
+            asc = work.tile([P, 2, Q], U8, align_bytes=64)
+            st[("ac", g)] = (ac, asc)
             nc.vector.quantize_mx(
-                out=ac[:].bitcast(FP8X4),
-                scales=asc[:],
-                in_=st[("grp", n)][:].rearrange("p q t -> p (q t)"),
+                out=ac[:, 0:k].rearrange("p j q -> p (j q)").bitcast(FP8X4),
+                scales=asc[:, 0:k].rearrange("p j q -> p (j q)"),
+                in_=st[("grp", g)][:, 0:k].rearrange("p j q t -> p (j q t)"),
             )
 
-        def read_out(n):
-            if n % 2 == 0:
-                mo = ps_mo.tile([P, 2, Q], F32)
-                st[("mo", n // 2)] = mo
-            ac, asc = st[("ac", n)]
-            nc.tensor.matmul_mx(
-                out=st[("mo", n // 2)][:, n % 2, :],
-                lhsT=vcodes[:, n, :].bitcast(FP8X4),
-                lhsT_scale=vscales[:, n, :],
-                rhs=ac[:].bitcast(FP8X4),
-                rhs_scale=asc[:],
-                start=True,
-                stop=True,
-            )
+        def read_out(g):
+            mo = ps_mo.tile([P, 2, Q], F32)
+            st[("mo", g)] = mo
+            ac, asc = st[("ac", g)]
+            for j in range(len(GROUPS[g])):
+                n = GROUPS[g][j]
+                nc.tensor.matmul_mx(
+                    out=mo[:, j, :],
+                    lhsT=vcodes[:, n, :].bitcast(FP8X4),
+                    lhsT_scale=vscales[:, n, :],
+                    rhs=ac[:, j, :].bitcast(FP8X4),
+                    rhs_scale=asc[:, j, :],
+                    start=True,
+                    stop=True,
+                )
 
         def cast_head():
             qv_t, i = place[("qv", 0)]
@@ -203,7 +228,7 @@ def tile_stm_head_t_kernel(tc, q_key, q_val, m_key, m_val, out):
             nc.gpsimd.tensor_scalar(out=qf4[:], in0=qv_t[:], scalar1=1.0, scalar2=0.0, op0=ALU.mult, op1=ALU.add)
             nc.sync.dma_start(out=out_d[:, 0:QC, 0, :], in_=qf4[:])
 
-        def cast(pr, on_vector=False):
+        def cast(pr, on_vector):
             qv_t, i = place[("qv", 2 * pr)]
             qf = outs.tile([P, 2, Q], F32)
             if on_vector:
@@ -212,68 +237,81 @@ def tile_stm_head_t_kernel(tc, q_key, q_val, m_key, m_val, out):
                 nc.scalar.copy(out=qf[:], in_=qv_t[:, i:i + 2, :])
             nc.sync.dma_start(out=out_d[:, 2 * pr:2 * pr + 2, 0, :], in_=qf[:])
 
-        def finish(pr):
+        def finish(g):
+            k = len(GROUPS[g])
+            n = GROUPS[g][0]
             res = outs.tile([P, 2, Q], F32)
-            nc.scalar.copy(out=res[:], in_=st[("mo", pr)][:])
-            nc.sync.dma_start(out=out_d[:, 2 * pr:2 * pr + 2, 1, :], in_=res[:])
-
-        def finish_one(n):
-            last = outs.tile([P, Q], F32)
-            nc.scalar.copy(out=last[:], in_=st[("mo", n // 2)][:, n % 2, :])
-            nc.sync.dma_start(out=out_d[:, n, 1, :], in_=last[:])
-
-        def share(n):
-            return GQ_LAST if n >= N - 2 else GQ
+            nc.scalar.copy(out=res[:, 0:k], in_=st[("mo", g)][:, 0:k])
+            nc.sync.dma_start(out=out_d[:, n:n + k, 1, :], in_=res[:, 0:k])
 
         later = list(range(FIRST, len(CHUNKS)))
-        LASTP = N // 2 - 1
         cast_head()
-        for s in range(-3, N + 2):
-            if 0 <= s - 1 < N:
-                read_out(s - 1)
-            if 0 <= s + 3 < N:
-                affinity(s + 3)
-            if s == -2:
-                flip_out(0)
-            if 0 <= s + 1 < N:
-                exps(s + 1)
-            if (s + 2) % 2 == 0 and 1 <= (s + 2) // 2 < N // 2:
-                flip_out((s + 2) // 2)
-            if (s - 2) % 2 == 0 and 0 <= (s - 2) // 2 < LASTP:
-                finish((s - 2) // 2)
-                if ((s - 2) // 2) % 2 == 0 and later:
+        affinity(0, 0)
+        affinity(0, 1)
+        flip(0)
+        affinity(1, 0)
+        affinity(1, 1)
+        affinity(2, 0)
+        maxima(0)
+        shift(0)
+        maxima(1)
+        shift(1)
+        flip_out(0)
+        exps(0, 0)
+        for g in range(LAST + 1):
+            pair = len(GROUPS[g]) > 1
+            nxt = g + 1 <= LAST
+            second = GROUPS[g + 1][1] if nxt and len(GROUPS[g + 1]) > 1 else None
+            first = GROUPS[g + 2][0] if g + 2 <= LAST else None
+            fourth = GROUPS[g + 2][1] if g + 2 <= LAST and len(GROUPS[g + 2]) > 1 else None
+            new_grp(g)
+            recip(g)
+            spread(g, 0)
+            if g >= 1:
+                quant(g - 1)
+                read_out(g - 1)
+            gpsimd_share(g, 0)
+            if pair:
+                gpsimd_share(g, 1)
+            if nxt:
+                flip(g + 1)
+                exps(g + 1, 0)
+            if second is not None:
+                if g == 0:
+                    affinity(second, 1)
+                maxima(second)
+            vector_share(g, 0)
+            if second is not None:
+                shift(second)
+                exps(g + 1, 1)
+            if first is not None:
+                if g == 0:
+                    affinity(first, 0)
+                affinity(first, 1)
+            if pair:
+                spread(g, 1)
+            if fourth is not None:
+                affinity(fourth, 0)
+                affinity(fourth, 1)
+            if g + 3 <= LAST:
+                affinity(GROUPS[g + 3][0], 0)
+            if g >= 1:
+                finish(g - 1)
+                if g % 2 == 1 and later:
                     ci = later.pop(0)
                     load(ci, ["mk", "qk", "mv"])
                     load_qv(ci - 2)
-            if s == N:
-                finish_one(N - 2)
-            for pr in CASTS.get(s, []):
-                cast(pr)
-            if s == N + 1:
-                finish_one(N - 1)
-            if s == -3:
-                flip(0)
-            if (s + 3) % 2 == 0 and 1 <= (s + 3) // 2 < N // 2:
-                flip((s + 3) // 2)
-            if 0 <= s + 2 < N:
-                maxima(s + 2, 0)
-                maxima(s + 2, 1)
-            if 0 <= s < N:
-                normalise(nc.vector, s, 0, Q - share(s), st[("rsp", s)])
-            if 0 <= s + 2 < N:
-                shift(s + 2)
-            if s == 0:
-                flip_quant(0)
-            if 0 <= s and s + 1 < N:
-                flip_quant(s + 1)
-            if 0 <= s + 1 < N:
-                recip(s + 1)
-            if 0 <= s < N:
-                quant(s)
-            for pr in VCASTS.get(s, []):
-                cast(pr, True)
-            if 0 <= s + 1 < N:
-                grp = work.tile([P, Q, 4], BF16, align_bytes=64)
-                st[("grp", s + 1)] = grp
-                if share(s + 1):
-                    normalise(nc.gpsimd, s + 1, Q - share(s + 1), Q, st[("rs", s + 1)])
+            if nxt:
+                flip_out(g + 1)
+            if first is not None:
+                maxima(first)
+            if pair:
+                vector_share(g, 1)
+            if first is not None:
+                shift(first)
+            flip_quant(g)
+            if 2 <= g + 1 < N // 2:
+                cast(g + 1, g in V_CASTS)
+        quant(LAST)
+        read_out(LAST)
+        finish(LAST)

@@ -18,16 +18,15 @@ SCALE = 128 ** -0.5
 FLOPS = 2 * (2 * N * Q * M * C)
 CHUNKS = [1, 1, 2, 4, 4, 4, 4, 4, 4, 4]
 FIRST = 5
-HEAD_LOADS = [(0, ["mk", "qk"]), (0, ["mv"]), (1, ["mk", "qk"]), (1, ["mv"]), (-1, 0), (2, ["mk", "qk", "mv"]), (3, ["mk", "qk", "mv"]), (-1, 1), (4, ["mk", "qk", "mv"]), (-1, 2)]
-GROUPS = [[0]] + [[n, n + 1] for n in range(1, N - 1, 2)] + [[N - 1]]
+HEAD_LOADS = [(0, ["mk", "qk"]), (1, ["mk", "qk"]), (2, ["mk", "qk"]), (0, ["mv"]), (1, ["mv"]), (-1, 0), (2, ["mv"]), (3, ["mk", "qk", "mv"]), (-1, 1), (4, ["mk", "qk", "mv"]), (-1, 2)]
+GROUPS = [[0]] + [[n, n + 1] for n in range(1, N - 3, 2)] + [[n] for n in range(N - 3, N)]
 LAST = len(GROUPS) - 1
 GQ = 160
-GQ_LAST = 0
 RUN = 4
 PAD = 80
 RING = 4
 QC = 4
-V_CASTS = [1, 3, 5, 7, 9, 11, 13]
+V_CASTS = [2, 4, 6, 8, 10, 12]
 
 
 def tile_stm_head_t_kernel(tc, q_key, q_val, m_key, m_val, out):
@@ -91,7 +90,7 @@ def tile_stm_head_t_kernel(tc, q_key, q_val, m_key, m_val, out):
         st = {}
 
         def share(g):
-            return GQ_LAST if g >= LAST else GQ
+            return GQ if g <= LAST - 2 else 0
 
         def affinity(n, u):
             mk_t, i = place[("mk", n)]
@@ -107,42 +106,40 @@ def tile_stm_head_t_kernel(tc, q_key, q_val, m_key, m_val, out):
                     stop=True,
                 )
 
-        def flip(g):
+        def flip(pr):
             xt = ps_xt.tile([P, 2, 2, C], F32)
-            st[("xt", g)] = xt
-            for j in range(len(GROUPS[g])):
-                mv_t, i = place[("mv", GROUPS[g][j])]
+            st[("xt", pr)] = xt
+            for j in range(2):
+                mv_t, i = place[("mv", 2 * pr + j)]
                 words = mv_t[:].bitcast(F32)
                 for u in range(2):
                     nc.tensor.transpose(xt[:, j, u, :], words[:, i, 128 * u:128 * (u + 1)], ident[:])
 
-        def flip_out(g):
-            k = len(GROUPS[g])
+        def flip_out(pr):
             vgrp = work.tile([P, 2, C, 4], BF16, align_bytes=64)
-            st[("vgrp", g)] = vgrp
-            nc.scalar.copy(
-                out=vgrp[:, 0:k].bitcast(F32), in_=st[("xt", g)][:, 0:k].rearrange("p j u c -> p j c u")
-            )
+            st[("vgrp", pr)] = vgrp
+            nc.scalar.copy(out=vgrp[:].bitcast(F32), in_=st[("xt", pr)][:].rearrange("p j u c -> p j c u"))
 
-        def flip_quant(g):
-            k = len(GROUPS[g])
-            n = GROUPS[g][0]
+        def flip_quant(pr):
+            pair = slice(2 * pr, 2 * pr + 2)
             nc.vector.quantize_mx(
-                out=vcodes[:, n:n + k, :].rearrange("p j c -> p (j c)").bitcast(FP8X4),
-                scales=vscales[:, n:n + k, :].rearrange("p j c -> p (j c)"),
-                in_=st[("vgrp", g)][:, 0:k].rearrange("p j c t -> p (j c t)"),
+                out=vcodes[:, pair, :].rearrange("p j c -> p (j c)").bitcast(FP8X4),
+                scales=vscales[:, pair, :].rearrange("p j c -> p (j c)"),
+                in_=st[("vgrp", pr)][:].rearrange("p j c t -> p (j c t)"),
             )
 
-        def maxima(n):
-            for u in range(2):
-                nc.vector.tensor_reduce(
-                    out=mxs[:, n % RING, 2 * u:2 * u + 2, 0], in_=st[("aff", n, u)][:], axis=AX.X, op=ALU.max
-                )
+        def maxima(n, u):
+            nc.vector.tensor_reduce(
+                out=mxs[:, n % RING, 2 * u:2 * u + 2, 0], in_=st[("aff", n, u)][:], axis=AX.X, op=ALU.max
+            )
 
-        def shift(n):
-            nb = small.tile([P, 4], F32)
-            st[("nb", n)] = nb
-            nc.vector.tensor_reduce(out=nb[:], in_=mxs[:, n % RING], axis=AX.X, op=ALU.mult)
+        def shift(n, t0=0, t1=4):
+            if t0 == 0:
+                nb = small.tile([P, 4], F32)
+                st[("nb", n)] = nb
+            nc.vector.tensor_reduce(
+                out=st[("nb", n)][:, t0:t1], in_=mxs[:, n % RING, t0:t1, :], axis=AX.X, op=ALU.mult
+            )
 
         def exps(g, j):
             n = GROUPS[g][j]
@@ -246,72 +243,144 @@ def tile_stm_head_t_kernel(tc, q_key, q_val, m_key, m_val, out):
 
         later = list(range(FIRST, len(CHUNKS)))
         cast_head()
-        affinity(0, 0)
-        affinity(0, 1)
+        def shares(g):
+            for j in range(len(GROUPS[g])):
+                gpsimd_share(g, j)
+
+        def load_later(g):
+            if g % 2 == 1 and later:
+                ci = later.pop(0)
+                load(ci, ["mk", "qk", "mv"])
+                load_qv(ci - 2)
+
+        for n in (0, 1):
+            affinity(n, 0)
+            affinity(n, 1)
         flip(0)
-        affinity(1, 0)
-        affinity(1, 1)
         affinity(2, 0)
-        maxima(0)
-        shift(0)
-        maxima(1)
+        affinity(2, 1)
+        maxima(0, 0)
+        maxima(0, 1)
+        shift(0, 0, 2)
+        maxima(1, 0)
+        shift(0, 2, 4)
+        maxima(1, 1)
+        maxima(2, 0)
         shift(1)
-        flip_out(0)
         exps(0, 0)
-        for g in range(LAST + 1):
-            pair = len(GROUPS[g]) > 1
-            nxt = g + 1 <= LAST
-            second = GROUPS[g + 1][1] if nxt and len(GROUPS[g + 1]) > 1 else None
-            first = GROUPS[g + 2][0] if g + 2 <= LAST else None
-            fourth = GROUPS[g + 2][1] if g + 2 <= LAST and len(GROUPS[g + 2]) > 1 else None
+        flip_out(0)
+        new_grp(0)
+        recip(0)
+        spread(0, 0)
+        shares(0)
+        flip(1)
+        exps(1, 0)
+        maxima(2, 1)
+        vector_share(0, 0)
+        shift(2)
+        exps(1, 1)
+        affinity(3, 0)
+        affinity(3, 1)
+        affinity(4, 0)
+        affinity(4, 1)
+        affinity(5, 0)
+        flip_out(1)
+        maxima(3, 0)
+        maxima(3, 1)
+        shift(3)
+        flip_quant(0)
+        cast(2, 0 in V_CASTS)
+
+        for g in range(1, LAST - 2):
+            second = GROUPS[g + 1][1] if len(GROUPS[g + 1]) > 1 else None
+            first = GROUPS[g + 2][0]
+            fourth = GROUPS[g + 2][1] if len(GROUPS[g + 2]) > 1 else None
             new_grp(g)
             recip(g)
             spread(g, 0)
-            if g >= 1:
-                quant(g - 1)
-                read_out(g - 1)
-            gpsimd_share(g, 0)
-            if pair:
-                gpsimd_share(g, 1)
-            if nxt:
-                flip(g + 1)
-                exps(g + 1, 0)
+            spread(g, 1)
+            quant(g - 1)
+            read_out(g - 1)
+            shares(g)
+            flip(g + 1)
+            exps(g + 1, 0)
             if second is not None:
-                if g == 0:
-                    affinity(second, 1)
-                maxima(second)
+                maxima(second, 0)
+                maxima(second, 1)
             vector_share(g, 0)
             if second is not None:
                 shift(second)
                 exps(g + 1, 1)
-            if first is not None:
-                if g == 0:
-                    affinity(first, 0)
-                affinity(first, 1)
-            if pair:
-                spread(g, 1)
+            affinity(first, 1)
             if fourth is not None:
                 affinity(fourth, 0)
                 affinity(fourth, 1)
-            if g + 3 <= LAST:
-                affinity(GROUPS[g + 3][0], 0)
-            if g >= 1:
-                finish(g - 1)
-                if g % 2 == 1 and later:
-                    ci = later.pop(0)
-                    load(ci, ["mk", "qk", "mv"])
-                    load_qv(ci - 2)
-            if nxt:
-                flip_out(g + 1)
-            if first is not None:
-                maxima(first)
-            if pair:
-                vector_share(g, 1)
-            if first is not None:
-                shift(first)
+            affinity(GROUPS[g + 3][0], 0)
+            finish(g - 1)
+            load_later(g)
+            flip_out(g + 1)
+            maxima(first, 0)
+            maxima(first, 1)
+            vector_share(g, 1)
+            shift(first)
             flip_quant(g)
-            if 2 <= g + 1 < N // 2:
-                cast(g + 1, g in V_CASTS)
-        quant(LAST)
-        read_out(LAST)
-        finish(LAST)
+            if g + 2 < N // 2:
+                cast(g + 2, g in V_CASTS)
+
+        g = LAST - 2
+        affinity(N - 1, 1)
+        new_grp(g)
+        recip(g)
+        spread(g, 0)
+        shares(g)
+        exps(g + 1, 0)
+        maxima(N - 1, 0)
+        maxima(N - 1, 1)
+        vector_share(g, 0)
+        shift(N - 1)
+        quant(g - 1)
+        read_out(g - 1)
+        flip_quant(g)
+        exps(g + 2, 0)
+        finish(g - 1)
+        g = LAST - 1
+        new_grp(g)
+        recip(g)
+        spread(g, 0)
+        shares(g)
+        quant(g - 1)
+        read_out(g - 1)
+        finish(g - 1)
+        vector_share(g, 0)
+        g = LAST
+        new_grp(g)
+        recip(g)
+        quant(g - 1)
+        read_out(g - 1)
+        finish(g - 1)
+        mo = ps_mo.tile([P, 2, Q], F32)
+        st[("mo", g)] = mo
+        ac = work.tile([P, 2, Q], U32, align_bytes=64)
+        asc = work.tile([P, 2, Q], U8, align_bytes=64)
+        HALF = Q // 2
+        for h in range(2):
+            normalise(nc.vector, g, 0, HALF * h, HALF * (h + 1), rsw[:, g % RING])
+        for h in range(2):
+            cols = slice(HALF * h, HALF * (h + 1))
+            nc.vector.quantize_mx(
+                out=ac[:, 0, cols].bitcast(FP8X4),
+                scales=asc[:, 0, cols],
+                in_=st[("grp", g)][:, 0, cols].rearrange("p q t -> p (q t)"),
+            )
+            nc.tensor.matmul_mx(
+                out=mo[:, 0, cols],
+                lhsT=vcodes[:, N - 1, :].bitcast(FP8X4),
+                lhsT_scale=vscales[:, N - 1, :],
+                rhs=ac[:, 0, cols].bitcast(FP8X4),
+                rhs_scale=asc[:, 0, cols],
+                start=True,
+                stop=True,
+            )
+            res = outs.tile([P, 2, Q], F32)
+            nc.scalar.copy(out=res[:, 0, cols], in_=mo[:, 0, cols])
+            nc.sync.dma_start(out=out_d[:, N - 1, 1, cols], in_=res[:, 0, cols])

@@ -57,8 +57,7 @@ def tile_stm_head_t_kernel(tc, q_key, q_val, m_key, m_val, out):
         make_identity(nc, ident[:])
         rsw = keep.tile([P, RING, 2, PAD], F32, name="rsw")
         nc.vector.memset(rsw[:], 0.0)
-        mxs = keep.tile([P, RING, 4, 2], F32, name="mxs")
-        nc.vector.memset(mxs[:], -SCALE)
+        mxs = keep.tile([P, RING, 4], F32, name="mxs")
         vcodes = keep.tile([P, N, C], U32, name="vcodes", align_bytes=64)
         vscales = keep.tile([P, N, C], U8, name="vscales", align_bytes=64)
 
@@ -130,26 +129,24 @@ def tile_stm_head_t_kernel(tc, q_key, q_val, m_key, m_val, out):
 
         def maxima(n, u):
             nc.vector.tensor_reduce(
-                out=mxs[:, n % RING, 2 * u:2 * u + 2, 0], in_=st[("aff", n, u)][:], axis=AX.X, op=ALU.max
+                out=mxs[:, n % RING, 2 * u:2 * u + 2], in_=st[("aff", n, u)][:], axis=AX.X, op=ALU.max
             )
 
         def shift(n, t0=0, t1=4):
             if t0 == 0:
                 nb = small.tile([P, 4], F32)
                 st[("nb", n)] = nb
-            nc.vector.tensor_reduce(
-                out=st[("nb", n)][:, t0:t1], in_=mxs[:, n % RING, t0:t1, :], axis=AX.X, op=ALU.mult
-            )
+            nc.scalar.mul(out=st[("nb", n)][:, t0:t1], in_=mxs[:, n % RING, t0:t1], mul=-SCALE)
 
-        def exps(g, j):
+        def exps(g, j, ts=range(4)):
             n = GROUPS[g][j]
-            if j == 0:
+            if j == 0 and ts[0] == 0:
                 sums = small.tile([P, 2, 4], F32)
                 ex = work.tile([P, 2, 4, Q], F32)
                 st[("sums", g)] = sums
                 st[("ex", g)] = ex
             nb = st[("nb", n)]
-            for t in range(4):
+            for t in ts:
                 nc.scalar.activation(
                     out=st[("ex", g)][:, j, t, :],
                     in_=st[("aff", n, t // 2)][:, t % 2, :],
@@ -261,33 +258,35 @@ def tile_stm_head_t_kernel(tc, q_key, q_val, m_key, m_val, out):
         affinity(2, 1)
         maxima(0, 0)
         maxima(0, 1)
-        shift(0, 0, 2)
         maxima(1, 0)
-        shift(0, 2, 4)
         maxima(1, 1)
         maxima(2, 0)
+        shift(0, 0, 2)
+        exps(0, 0, [0])
+        shift(0, 2, 4)
+        exps(0, 0, [1, 2, 3])
         shift(1)
-        exps(0, 0)
         flip_out(0)
         new_grp(0)
         recip(0)
         spread(0, 0)
         shares(0)
         flip(1)
-        exps(1, 0)
+        exps(1, 0, [0, 1, 2])
         maxima(2, 1)
-        vector_share(0, 0)
         shift(2)
+        exps(1, 0, [3])
+        vector_share(0, 0)
         exps(1, 1)
         affinity(3, 0)
         affinity(3, 1)
         affinity(4, 0)
         affinity(4, 1)
         affinity(5, 0)
-        flip_out(1)
         maxima(3, 0)
         maxima(3, 1)
         shift(3)
+        flip_out(1)
         flip_quant(0)
         cast(2, 0 in V_CASTS)
 
@@ -303,13 +302,14 @@ def tile_stm_head_t_kernel(tc, q_key, q_val, m_key, m_val, out):
             read_out(g - 1)
             shares(g)
             flip(g + 1)
-            exps(g + 1, 0)
+            exps(g + 1, 0, [0, 1, 2])
             if second is not None:
                 maxima(second, 0)
                 maxima(second, 1)
+                shift(second)
+            exps(g + 1, 0, [3])
             vector_share(g, 0)
             if second is not None:
-                shift(second)
                 exps(g + 1, 1)
             affinity(first, 1)
             if fourth is not None:
@@ -318,11 +318,11 @@ def tile_stm_head_t_kernel(tc, q_key, q_val, m_key, m_val, out):
             affinity(GROUPS[g + 3][0], 0)
             finish(g - 1)
             load_later(g)
-            flip_out(g + 1)
             maxima(first, 0)
             maxima(first, 1)
-            vector_share(g, 1)
             shift(first)
+            flip_out(g + 1)
+            vector_share(g, 1)
             flip_quant(g)
             if g + 2 < N // 2:
                 cast(g + 2, g in V_CASTS)
@@ -333,11 +333,12 @@ def tile_stm_head_t_kernel(tc, q_key, q_val, m_key, m_val, out):
         recip(g)
         spread(g, 0)
         shares(g)
-        exps(g + 1, 0)
+        exps(g + 1, 0, [0, 1, 2])
         maxima(N - 1, 0)
         maxima(N - 1, 1)
-        vector_share(g, 0)
         shift(N - 1)
+        exps(g + 1, 0, [3])
+        vector_share(g, 0)
         quant(g - 1)
         read_out(g - 1)
         flip_quant(g)

@@ -16,9 +16,9 @@ N, C, Q, M = 32, 128, 256, 512
 P = 128
 SCALE = 128 ** -0.5
 FLOPS = 2 * (2 * N * Q * M * C)
-CHUNKS = [1, 1, 2, 4, 4, 4, 4, 4, 4, 4]
-FIRST = 5
-HEAD_LOADS = [(0, ["mk", "qk"]), (1, ["mk", "qk"]), (2, ["mk", "qk"]), (0, ["mv"]), (1, ["mv"]), (-1, 0), (2, ["mv"]), (3, ["mk", "qk", "mv"]), (-1, 1), (4, ["mk", "qk", "mv"]), (-1, 2)]
+CHUNKS = [1, 1, 2, 2, 2, 4, 4, 4, 4, 4, 4]
+FIRST = 6
+HEAD_LOADS = [(0, ["mk", "qk"]), (1, ["mk", "qk"]), (2, ["mk", "qk"]), (0, ["mv"]), (1, ["mv"]), (3, ["mk", "qk"]), (2, ["mv"]), (-1, 0), (4, ["mk", "qk"]), (3, ["mv"]), (-1, 1), (4, ["mv"]), (5, ["mk", "qk", "mv"]), (-1, 2)]
 GROUPS = [[0]] + [[n, n + 1] for n in range(1, N - 3, 2)] + [[n] for n in range(N - 3, N)]
 LAST = len(GROUPS) - 1
 GQ = 160
@@ -26,7 +26,8 @@ RUN = 4
 PAD = 80
 RING = 4
 QC = 4
-V_CASTS = [2, 4, 6, 8, 10, 12]
+G_CASTS = [0]
+V_CASTS = [3, 5, 7, 9, 11, 13]
 
 
 def tile_stm_head_t_kernel(tc, q_key, q_val, m_key, m_val, out):
@@ -216,16 +217,14 @@ def tile_stm_head_t_kernel(tc, q_key, q_val, m_key, m_val, out):
                     stop=True,
                 )
 
-        def cast_head():
-            qv_t, i = place[("qv", 0)]
-            qf4 = keep.tile([P, QC, Q], F32, name="qf4")
-            nc.gpsimd.tensor_scalar(out=qf4[:], in0=qv_t[:], scalar1=1.0, scalar2=0.0, op0=ALU.mult, op1=ALU.add)
-            nc.sync.dma_start(out=out_d[:, 0:QC, 0, :], in_=qf4[:])
-
-        def cast(pr, on_vector):
+        def cast(pr):
             qv_t, i = place[("qv", 2 * pr)]
             qf = outs.tile([P, 2, Q], F32)
-            if on_vector:
+            if pr in G_CASTS:
+                nc.gpsimd.tensor_scalar(
+                    out=qf[:], in0=qv_t[:, i:i + 2, :], scalar1=1.0, scalar2=0.0, op0=ALU.mult, op1=ALU.add
+                )
+            elif pr in V_CASTS:
                 nc.vector.tensor_copy(out=qf[:], in_=qv_t[:, i:i + 2, :])
             else:
                 nc.scalar.copy(out=qf[:], in_=qv_t[:, i:i + 2, :])
@@ -239,7 +238,6 @@ def tile_stm_head_t_kernel(tc, q_key, q_val, m_key, m_val, out):
             nc.sync.dma_start(out=out_d[:, n:n + k, 1, :], in_=res[:, 0:k])
 
         later = list(range(FIRST, len(CHUNKS)))
-        cast_head()
         def shares(g):
             for j in range(len(GROUPS[g])):
                 gpsimd_share(g, j)
@@ -248,7 +246,7 @@ def tile_stm_head_t_kernel(tc, q_key, q_val, m_key, m_val, out):
             if g % 2 == 1 and later:
                 ci = later.pop(0)
                 load(ci, ["mk", "qk", "mv"])
-                load_qv(ci - 2)
+                load_qv(ci - 3)
 
         for n in (0, 1):
             affinity(n, 0)
@@ -271,6 +269,7 @@ def tile_stm_head_t_kernel(tc, q_key, q_val, m_key, m_val, out):
         recip(0)
         spread(0, 0)
         shares(0)
+        cast(0)
         flip(1)
         exps(1, 0, [0, 1, 2])
         maxima(2, 1)
@@ -288,7 +287,7 @@ def tile_stm_head_t_kernel(tc, q_key, q_val, m_key, m_val, out):
         shift(3)
         flip_out(1)
         flip_quant(0)
-        cast(2, 0 in V_CASTS)
+        cast(1)
 
         for g in range(1, LAST - 2):
             second = GROUPS[g + 1][1] if len(GROUPS[g + 1]) > 1 else None
@@ -324,8 +323,8 @@ def tile_stm_head_t_kernel(tc, q_key, q_val, m_key, m_val, out):
             flip_out(g + 1)
             vector_share(g, 1)
             flip_quant(g)
-            if g + 2 < N // 2:
-                cast(g + 2, g in V_CASTS)
+            if g + 1 < N // 2:
+                cast(g + 1)
 
         g = LAST - 2
         affinity(N - 1, 1)
@@ -359,8 +358,7 @@ def tile_stm_head_t_kernel(tc, q_key, q_val, m_key, m_val, out):
         quant(g - 1)
         read_out(g - 1)
         finish(g - 1)
-        mo = ps_mo.tile([P, 2, Q], F32)
-        st[("mo", g)] = mo
+        aff = ps_aff.tile([P, 2, Q], F32)
         ac = work.tile([P, 2, Q], U32, align_bytes=64)
         asc = work.tile([P, 2, Q], U8, align_bytes=64)
         HALF = Q // 2
@@ -374,7 +372,7 @@ def tile_stm_head_t_kernel(tc, q_key, q_val, m_key, m_val, out):
                 in_=st[("grp", g)][:, 0, cols].rearrange("p q t -> p (q t)"),
             )
             nc.tensor.matmul_mx(
-                out=mo[:, 0, cols],
+                out=aff[:, 0, cols],
                 lhsT=vcodes[:, N - 1, :].bitcast(FP8X4),
                 lhsT_scale=vscales[:, N - 1, :],
                 rhs=ac[:, 0, cols].bitcast(FP8X4),
@@ -383,5 +381,5 @@ def tile_stm_head_t_kernel(tc, q_key, q_val, m_key, m_val, out):
                 stop=True,
             )
             res = outs.tile([P, 2, Q], F32)
-            nc.scalar.copy(out=res[:, 0, cols], in_=mo[:, 0, cols])
+            nc.scalar.copy(out=res[:, 0, cols], in_=aff[:, 0, cols])
             nc.sync.dma_start(out=out_d[:, N - 1, 1, cols], in_=res[:, 0, cols])

from contextlib import ExitStack

import concourse.mybir as mybir
from concourse.masks import make_identity

FP8X4 = mybir.dt.float8_e4m3fn_x4
BF16 = mybir.dt.bfloat16
F32 = mybir.dt.float32
U32 = mybir.dt.uint32
U8 = mybir.dt.uint8
ALU = mybir.AluOpType
ACT = mybir.ActivationFunctionType
AX = mybir.AxisListType

N, C, Q, M = 32, 128, 256, 512
P = 128
SCALE = 128 ** -0.5
FLOPS = 2 * (2 * N * Q * M * C)
CHUNKS = [1, 1, 2, 2, 2, 4, 4, 4, 4, 4, 4]
FIRST = 6
HEAD_LOADS = [(0, ["mk", "qk"]), (1, ["mk", "qk"]), (2, ["mk", "qk"]), (0, ["mv"]), (1, ["mv"]), (3, ["mk", "qk"]), (2, ["mv"]), (-1, 0), (4, ["mk", "qk"]), (3, ["mv"]), (-1, 1), (4, ["mv"]), (5, ["mk", "qk", "mv"]), (-1, 2)]
GROUPS = [[0]] + [[n, n + 1] for n in range(1, N - 3, 2)] + [[n] for n in range(N - 3, N)]
LAST = len(GROUPS) - 1
GQ = 160
RUN = 4
PAD = 80
RING = 4
QC = 4
G_CASTS = [0]
V_CASTS = [3, 5, 7, 9, 11, 13]


def tile_stm_head_t_kernel(tc, q_key, q_val, m_key, m_val, out):
    nc = tc.nc
    qk_d = q_key.rearrange("n c h w -> c n (h w)")
    qv_d = q_val.rearrange("n c h w -> c n (h w)")
    mk_d = m_key.rearrange("n c t h w -> c n (t h w)")
    mv_d = m_val.rearrange("n c t h w -> c n (t h w)")
    out_d = out.rearrange("n (g c) h w -> c n g (h w)", g=2)

    with ExitStack() as ctx:
        keep = ctx.enter_context(tc.tile_pool(name="keep", bufs=1))
        work = ctx.enter_context(tc.tile_pool(name="work", bufs=3))
        outs = ctx.enter_context(tc.tile_pool(name="outs", bufs=4))
        small = ctx.enter_context(tc.tile_pool(name="small", bufs=6))
        ps_aff = ctx.enter_context(tc.psum_pool(name="ps_aff", bufs=5))
        ps_xt = ctx.enter_context(tc.psum_pool(name="ps_xt", bufs=1))
        ps_mo = ctx.enter_context(tc.psum_pool(name="ps_mo", bufs=1))
        ps_rs = ctx.enter_context(tc.psum_pool(name="ps_rs", bufs=1))
        ctx.enter_context(tc.manual_schedule())

        zero = keep.tile([P, 1], F32, name="zero")
        one = keep.tile([P, 1], F32, name="one")
        nc.vector.memset(zero[:], 0.0)
        nc.scalar.activation(out=one[:], in_=zero[:], func=ACT.Exp)

        ident = keep.tile([P, P], F32, name="ident")
        make_identity(nc, ident[:])
        rsw = keep.tile([P, RING, 2, PAD], F32, name="rsw")
        nc.vector.memset(rsw[:], 0.0)
        mxs = keep.tile([P, RING, 4], F32, name="mxs")
        vcodes = keep.tile([P, N, C], U32, name="vcodes", align_bytes=64)
        vscales = keep.tile([P, N, C], U8, name="vscales", align_bytes=64)

        starts = [sum(CHUNKS[:ci]) for ci in range(len(CHUNKS))]
        place = {}

        def load(ci, kinds):
            size = CHUNKS[ci]
            n0 = starts[ci]
            for kind in kinds:
                src, width = {"mk": (mk_d, M), "qk": (qk_d, Q), "mv": (mv_d, M)}[kind]
                t = keep.tile([P, size, width], BF16, name="%s%d" % (kind, ci))
                nc.sync.dma_start(out=t[:], in_=src[:, n0:n0 + size, :])
                for i in range(size):
                    place[(kind, n0 + i)] = (t, i)

        def load_qv(j):
            t = keep.tile([P, QC, Q], BF16, name="qv%d" % j)
            nc.sync.dma_start(out=t[:], in_=qv_d[:, QC * j:QC * (j + 1), :])
            for i in range(QC):
                place[("qv", QC * j + i)] = (t, i)

        for ci, kinds in HEAD_LOADS:
            if ci < 0:
                load_qv(kinds)
            else:
                load(ci, kinds)

        st = {}

        def share(g):
            return GQ if g <= LAST - 2 else 0

        def affinity(n, u):
            mk_t, i = place[("mk", n)]
            qk_t, i = place[("qk", n)]
            aff = ps_aff.tile([P, 2, Q], F32)
            st[("aff", n, u)] = aff
            for b in range(2):
                nc.tensor.matmul(
                    out=aff[:, b, :],
                    lhsT=mk_t[:, i, 256 * u + b:256 * (u + 1):2],
                    rhs=qk_t[:, i, :],
                    start=True,
                    stop=True,
                )

        def flip(pr):
            xt = ps_xt.tile([P, 2, 2, C], F32)
            st[("xt", pr)] = xt
            for j in range(2):
                mv_t, i = place[("mv", 2 * pr + j)]
                words = mv_t[:].bitcast(F32)
                for u in range(2):
                    nc.tensor.transpose(xt[:, j, u, :], words[:, i, 128 * u:128 * (u + 1)], ident[:])

        def flip_out(pr):
            vgrp = work.tile([P, 2, C, 4], BF16, align_bytes=64)
            st[("vgrp", pr)] = vgrp
            nc.scalar.copy(out=vgrp[:].bitcast(F32), in_=st[("xt", pr)][:].rearrange("p j u c -> p j c u"))

        def flip_quant(pr):
            pair = slice(2 * pr, 2 * pr + 2)
            nc.vector.quantize_mx(
                out=vcodes[:, pair, :].rearrange("p j c -> p (j c)").bitcast(FP8X4),
                scales=vscales[:, pair, :].rearrange("p j c -> p (j c)"),
                in_=st[("vgrp", pr)][:].rearrange("p j c t -> p (j c t)"),
            )

        def maxima(n, u):
            nc.vector.tensor_reduce(
                out=mxs[:, n % RING, 2 * u:2 * u + 2], in_=st[("aff", n, u)][:], axis=AX.X, op=ALU.max
            )

        def shift(n, t0=0, t1=4):
            if t0 == 0:
                nb = small.tile([P, 4], F32)
                st[("nb", n)] = nb
            nc.scalar.mul(out=st[("nb", n)][:, t0:t1], in_=mxs[:, n % RING, t0:t1], mul=-SCALE)

        def exps(g, j, ts=range(4)):
            n = GROUPS[g][j]
            if j == 0 and ts[0] == 0:
                sums = small.tile([P, 2, 4], F32)
                ex = work.tile([P, 2, 4, Q], F32)
                st[("sums", g)] = sums
                st[("ex", g)] = ex
            nb = st[("nb", n)]
            for t in ts:
                nc.scalar.activation(
                    out=st[("ex", g)][:, j, t, :],
                    in_=st[("aff", n, t // 2)][:, t % 2, :],
                    func=ACT.Exp,
                    bias=nb[:, t:t + 1],
                    scale=SCALE,
                    accum_out=st[("sums", g)][:, j, t:t + 1],
                )

        def recip(g):
            k = len(GROUPS[g])
            nc.vector.reciprocal(out=rsw[:, g % RING, 0:k, 0:4], in_=st[("sums", g)][:, 0:k, :])

        def spread(g, j):
            if share(g):
                if j == 0:
                    rsp = ps_rs.tile([P, 2, PAD], F32)
                    st[("rsp", g)] = rsp
                nc.tensor.matmul(
                    out=st[("rsp", g)][:, j, :], lhsT=ident[:], rhs=rsw[:, g % RING, j, :], start=True, stop=True
                )

        def new_grp(g):
            grp = work.tile([P, 2, Q, 4], BF16, align_bytes=64)
            st[("grp", g)] = grp

        def normalise(eng, g, j, q0, q1, factor):
            eng.tensor_tensor(
                out=st[("grp", g)][:, j, q0:q1, :].rearrange("p (c i) t -> p c t i", i=RUN),
                in0=st[("ex", g)][:, j, :, q0:q1].rearrange("p t (c i) -> p c t i", i=RUN),
                in1=factor[:, j, 0:4].unsqueeze(1).unsqueeze(3).to_broadcast([P, (q1 - q0) // RUN, 4, RUN]),
                op=ALU.mult,
            )

        def vector_share(g, j):
            factor = st[("rsp", g)] if share(g) else rsw[:, g % RING]
            normalise(nc.vector, g, j, 0, Q - share(g), factor)

        def gpsimd_share(g, j):
            if share(g):
                normalise(nc.gpsimd, g, j, Q - share(g), Q, rsw[:, g % RING])

        def quant(g):
            k = len(GROUPS[g])
            ac = work.tile([P, 2, Q], U32, align_bytes=64)
            asc = work.tile([P, 2, Q], U8, align_bytes=64)
            st[("ac", g)] = (ac, asc)
            nc.vector.quantize_mx(
                out=ac[:, 0:k].rearrange("p j q -> p (j q)").bitcast(FP8X4),
                scales=asc[:, 0:k].rearrange("p j q -> p (j q)"),
                in_=st[("grp", g)][:, 0:k].rearrange("p j q t -> p (j q t)"),
            )

        def read_out(g):
            mo = ps_mo.tile([P, 2, Q], F32)
            st[("mo", g)] = mo
            ac, asc = st[("ac", g)]
            for j in range(len(GROUPS[g])):
                n = GROUPS[g][j]
                nc.tensor.matmul_mx(
                    out=mo[:, j, :],
                    lhsT=vcodes[:, n, :].bitcast(FP8X4),
                    lhsT_scale=vscales[:, n, :],
                    rhs=ac[:, j, :].bitcast(FP8X4),
                    rhs_scale=asc[:, j, :],
                    start=True,
                    stop=True,
                )

        def cast(pr):
            qv_t, i = place[("qv", 2 * pr)]
            qf = outs.tile([P, 2, Q], F32)
            if pr in G_CASTS:
                nc.gpsimd.tensor_scalar(
                    out=qf[:], in0=qv_t[:, i:i + 2, :], scalar1=1.0, scalar2=0.0, op0=ALU.mult, op1=ALU.add
                )
            elif pr in V_CASTS:
                nc.vector.tensor_copy(out=qf[:], in_=qv_t[:, i:i + 2, :])
            else:
                nc.scalar.copy(out=qf[:], in_=qv_t[:, i:i + 2, :])
            nc.sync.dma_start(out=out_d[:, 2 * pr:2 * pr + 2, 0, :], in_=qf[:])

        def finish(g):
            k = len(GROUPS[g])
            n = GROUPS[g][0]
            res = outs.tile([P, 2, Q], F32)
            nc.scalar.copy(out=res[:, 0:k], in_=st[("mo", g)][:, 0:k])
            nc.sync.dma_start(out=out_d[:, n:n + k, 1, :], in_=res[:, 0:k])

        later = list(range(FIRST, len(CHUNKS)))
        def shares(g):
            for j in range(len(GROUPS[g])):
                gpsimd_share(g, j)

        def load_later(g):
            if g % 2 == 1 and later:
                ci = later.pop(0)
                load(ci, ["mk", "qk", "mv"])
                load_qv(ci - 3)

        for n in (0, 1):
            affinity(n, 0)
            affinity(n, 1)
        flip(0)
        affinity(2, 0)
        affinity(2, 1)
        maxima(0, 0)
        maxima(0, 1)
        maxima(1, 0)
        maxima(1, 1)
        maxima(2, 0)
        shift(0, 0, 2)
        exps(0, 0, [0])
        shift(0, 2, 4)
        exps(0, 0, [1, 2, 3])
        shift(1)
        flip_out(0)
        new_grp(0)
        recip(0)
        spread(0, 0)
        shares(0)
        cast(0)
        flip(1)
        exps(1, 0, [0, 1, 2])
        maxima(2, 1)
        shift(2)
        exps(1, 0, [3])
        vector_share(0, 0)
        exps(1, 1)
        affinity(3, 0)
        affinity(3, 1)
        affinity(4, 0)
        affinity(4, 1)
        affinity(5, 0)
        maxima(3, 0)
        maxima(3, 1)
        shift(3)
        flip_out(1)
        flip_quant(0)
        cast(1)

        for g in range(1, LAST - 2):
            second = GROUPS[g + 1][1] if len(GROUPS[g + 1]) > 1 else None
            first = GROUPS[g + 2][0]
            fourth = GROUPS[g + 2][1] if len(GROUPS[g + 2]) > 1 else None
            new_grp(g)
            recip(g)
            spread(g, 0)
            spread(g, 1)
            quant(g - 1)
            read_out(g - 1)
            shares(g)
            flip(g + 1)
            exps(g + 1, 0, [0, 1, 2])
            if second is not None:
                maxima(second, 0)
                maxima(second, 1)
                shift(second)
            exps(g + 1, 0, [3])
            vector_share(g, 0)
            if second is not None:
                exps(g + 1, 1)
            affinity(first, 1)
            if fourth is not None:
                affinity(fourth, 0)
                affinity(fourth, 1)
            affinity(GROUPS[g + 3][0], 0)
            finish(g - 1)
            load_later(g)
            maxima(first, 0)
            maxima(first, 1)
            shift(first)
            flip_out(g + 1)
            vector_share(g, 1)
            flip_quant(g)
            if g + 1 < N // 2:
                cast(g + 1)

        g = LAST - 2
        affinity(N - 1, 1)
        new_grp(g)
        recip(g)
        spread(g, 0)
        shares(g)
        exps(g + 1, 0, [0, 1, 2])
        maxima(N - 1, 0)
        maxima(N - 1, 1)
        shift(N - 1)
        exps(g + 1, 0, [3])
        vector_share(g, 0)
        quant(g - 1)
        read_out(g - 1)
        flip_quant(g)
        exps(g + 2, 0)
        finish(g - 1)
        g = LAST - 1
        new_grp(g)
        recip(g)
        spread(g, 0)
        shares(g)
        quant(g - 1)
        read_out(g - 1)
        finish(g - 1)
        vector_share(g, 0)
        g = LAST
        new_grp(g)
        recip(g)
        quant(g - 1)
        read_out(g - 1)
        finish(g - 1)
        aff = ps_aff.tile([P, 2, Q], F32)
        ac = work.tile([P, 2, Q], U32, align_bytes=64)
        asc = work.tile([P, 2, Q], U8, align_bytes=64)
        HALF = Q // 2
        for h in range(2):
            normalise(nc.vector, g, 0, HALF * h, HALF * (h + 1), rsw[:, g % RING])
        for h in range(2):
            cols = slice(HALF * h, HALF * (h + 1))
            nc.vector.quantize_mx(
                out=ac[:, 0, cols].bitcast(FP8X4),
                scales=asc[:, 0, cols],
                in_=st[("grp", g)][:, 0, cols].rearrange("p q t -> p (q t)"),
            )
            nc.tensor.matmul_mx(
                out=aff[:, 0, cols],
                lhsT=vcodes[:, N - 1, :].bitcast(FP8X4),
                lhsT_scale=vscales[:, N - 1, :],
                rhs=ac[:, 0, cols].bitcast(FP8X4),
                rhs_scale=asc[:, 0, cols],
                start=True,
                stop=True,
            )
            res = outs.tile([P, 2, Q], F32)
            nc.scalar.copy(out=res[:, 0, cols], in_=aff[:, 0, cols])
            nc.sync.dma_start(out=out_d[:, N - 1, 1, cols], in_=res[:, 0, cols])
